import numpy as np
import ml_dtypes


def mxq(x, axis, fmt="e4m3"):
    dtype, down = {"e4m3": (ml_dtypes.float8_e4m3fn, 7), "e5m2": (ml_dtypes.float8_e5m2, 14)}[fmt]
    v = np.moveaxis(np.asarray(x, np.float32).astype(ml_dtypes.bfloat16).astype(np.float64), axis, -1)
    blocks = v.reshape(v.shape[:-1] + (-1, 32))
    amax = np.abs(blocks).max(-1, keepdims=True)
    byte = np.maximum(np.where(amax > 0, np.frexp(amax)[1] - 1 + 127, 0) - down, 1)
    scale = np.exp2(byte - 127.0)
    codes = (blocks / scale).astype(np.float32).astype(dtype).astype(np.float64)
    return np.moveaxis((codes * scale).reshape(v.shape), -1, axis)


WIDE = False


def mx_kscale(k):
    if not WIDE:
        return np.ones(k)
    levels = np.array([10, -10, 5, -5, 0])
    a = np.random.permutation(np.resize(levels, k // 512 * 4)).reshape(k // 512, 4)
    idx = np.arange(k)
    return np.exp2(a[idx // 512, idx % 128 // 32])


BF16 = ml_dtypes.bfloat16


def bf(x):
    return np.asarray(x, np.float32).astype(BF16)


def f64(x):
    return np.asarray(x).astype(np.float64)


E2M1 = np.array([0.0, 0.5, 1.0, 1.5, 2.0, 3.0, 4.0, 6.0, -0.0, -0.5, -1.0, -1.5, -2.0, -3.0, -4.0, -6.0])


def pack_weight(w, fmt):
    k, n = w.shape
    w = f64(bf(w)).reshape(k // 32, 32, n)
    amax = np.abs(w).max(1)
    if fmt == "e4m3":
        byte = np.frexp(amax)[1] - 1 + 127 - 7
    else:
        mant, ex = np.frexp(amax / 6.0)
        byte = np.where(mant > 0.5, ex, ex - 1) + 127
    byte = np.clip(np.where(amax > 0, byte, 1), 1, 254)
    scaled = (w * np.exp2(127.0 - byte)[:, None, :]).reshape(k, n).astype(np.float32)
    by_word = np.ascontiguousarray(scaled.reshape(k // 512, 128, 4, n).transpose(0, 1, 3, 2))
    if fmt == "e4m3":
        words = by_word.astype(ml_dtypes.float8_e4m3fn).view(np.uint8)
    else:
        c = by_word.astype(ml_dtypes.float4_e2m1fn).view(np.uint8) & 0xF
        words = c[..., 0::2] | (c[..., 1::2] << 4)
    return np.ascontiguousarray(words), np.ascontiguousarray(byte.astype(np.uint8).reshape(k // 512, 16, n))


def unpack_weight(words, scales, fmt):
    g, p, n, _ = words.shape
    if fmt == "e4m3":
        vals = np.ascontiguousarray(words).view(ml_dtypes.float8_e4m3fn).astype(np.float64)
    else:
        nib = np.empty((g, p, n, 4), np.uint8)
        nib[..., 0::2] = words & 0xF
        nib[..., 1::2] = words >> 4
        vals = E2M1[nib]
    vals = vals * np.repeat(np.exp2(scales.astype(np.float64) - 127.0), 8, axis=1)[..., None]
    return vals.transpose(0, 1, 3, 2).reshape(g * 512, n)


B, N, D0, D1, D2, D3 = 32, 128, 1024, 1024, 512, 1024
EPS = 1e-5


def batch_norm(x, g, b):
    mean = x.mean(axis=(0, 1))
    var = np.square(x - mean).mean(axis=(0, 1))
    return (x - mean) * (1.0 / np.sqrt(var + EPS)) * g + b


def setup_inputs():
    s = mx_kscale(D0)
    feats = np.random.standard_normal((B, N, D0)) * np.exp(0.4 * np.random.standard_normal(D0)) + 0.5 * np.random.standard_normal(D0)
    g0 = bf((1.0 + 0.2 * np.random.standard_normal(D0)) * s)
    b0 = bf(0.2 * np.random.standard_normal(D0) * s)
    W0 = np.random.standard_normal((D1, D0)) / np.sqrt(D0) / s
    W0_words, W0_scales = pack_weight(W0.T, "e4m3")
    return {"set_feats": bf(feats),
            "g0": g0,
            "b0": b0,
            "W0_words": W0_words,
            "W0_scales": W0_scales,
            "c0": bf(0.3 * np.random.standard_normal(D1)),
            "g1": bf(1.0 + 0.2 * np.random.standard_normal(D1)),
            "b1": bf(0.2 * np.random.standard_normal(D1))}


def reference(set_feats, g0, b0, W0_words, W0_scales, c0, g1, b1):
    x0 = batch_norm(f64(set_feats), f64(g0), f64(b0))
    h0 = np.maximum((mxq(x0, 2, "e4m3") @ unpack_weight(W0_words, W0_scales, "e4m3")) + f64(c0), 0.0)
    return batch_norm(h0, f64(g1), f64(b1))

@@ -1,0 +1,257 @@
+from concourse import mybir
+from concourse.masks import make_identity
+
+F32 = mybir.dt.float32
+BF16 = mybir.dt.bfloat16
+I32 = mybir.dt.int32
+U32 = mybir.dt.uint32
+U8 = mybir.dt.uint8
+FP8X4 = mybir.dt.float8_e4m3fn_x4
+ACT = mybir.ActivationFunctionType
+ALU = mybir.AluOpType
+
+P = 128
+PACK = 4
+K_PASS = P * PACK
+ROWS = 4096
+D_IN = 1024
+D_OUT = 1024
+PASSES = D_IN // K_PASS
+CHUNK = 512
+CHUNKS = ROWS // CHUNK
+ROW_TILES = CHUNK // P
+BLOCKS = D_OUT // P
+HALVES = 2
+BN_MAX = 512
+EPS = 1e-5
+
+FLOPS = 2 * ROWS * D_IN * D_OUT
+
+
+def norm_coefficients(nc, pool, mean, var, gain, shift, scale_out, bias_out, width):
+    std = pool.tile([P, width], F32)
+    nc.vector.tensor_scalar_add(out=std[:], in0=var, scalar1=EPS)
+    nc.scalar.activation(out=std[:], in_=std[:], func=ACT.Sqrt)
+    nc.vector.reciprocal(out=std[:], in_=std[:])
+    nc.vector.tensor_mul(out=scale_out, in0=gain, in1=std[:])
+    nc.vector.tensor_mul(out=std[:], in0=mean, in1=scale_out)
+    nc.vector.tensor_sub(out=bias_out, in0=shift, in1=std[:])
+
+
+def tile_settransform_pa_t_kernel(
+    tc, set_feats, g0, b0, W0_words, W0_scales, c0, g1, b1, out
+):
+    nc = tc.nc
+    x_view = set_feats.flatten_outer_dims().rearrange(
+        "(c p j) k -> c p j k", p=P, j=ROW_TILES
+    )
+    out_view = out.flatten_outer_dims().rearrange(
+        "(c p j) n -> c p j n", p=P, j=ROW_TILES
+    )
+
+    with tc.tile_pool(name="keep", bufs=1) as keep, tc.tile_pool(
+        name="xin", bufs=4
+    ) as xin, tc.tile_pool(name="stage", bufs=3) as stage, tc.tile_pool(
+        name="hidden", bufs=3
+    ) as hidden, tc.tile_pool(name="small", bufs=4) as small, tc.tile_pool(
+        name="outs", bufs=4
+    ) as outs, tc.psum_pool(name="psum", bufs=4) as psum:
+        warm = keep.tile([P, 1], F32)
+        nc.vector.memset(warm[:], 1.0)
+        nc.scalar.activation(out=warm[:], in_=warm[:], func=ACT.Sqrt)
+
+        ident_f32 = keep.tile([P, P], F32)
+        make_identity(nc, ident_f32[:])
+        ident_bf16 = keep.tile([P, P], BF16)
+        make_identity(nc, ident_bf16[:])
+
+        w_scales = keep.tile([P, PASSES, D_OUT], U8, align_bytes=64)
+        nc.vector.memset(w_scales[:].rearrange("p g n -> p (g n)").bitcast(I32), 0)
+        param_rows = keep.tile([P, P], BF16)
+        nc.vector.memset(param_rows[:], 0.0)
+
+        gain0_bf = keep.tile([P, PASSES, PACK], BF16)
+        shift0_bf = keep.tile([P, PASSES, PACK], BF16)
+        nc.scalar.dma_start(
+            out=gain0_bf[:], in_=g0.rearrange("(g p t) -> p g t", g=PASSES, p=P)
+        )
+        nc.scalar.dma_start(
+            out=shift0_bf[:], in_=b0.rearrange("(g p t) -> p g t", g=PASSES, p=P)
+        )
+        for v, vec in enumerate((c0, g1, b1)):
+            nc.scalar.dma_start(
+                out=param_rows[v * BLOCKS : (v + 1) * BLOCKS, :],
+                in_=vec.rearrange("(b p) -> b p", p=P),
+            )
+        gain0 = keep.tile([P, PASSES, PACK], F32)
+        shift0 = keep.tile([P, PASSES, PACK], F32)
+        nc.vector.tensor_copy(out=gain0[:], in_=gain0_bf[:])
+        nc.vector.tensor_copy(out=shift0[:], in_=shift0_bf[:])
+        params_ps = psum.tile([P, P], BF16, tag="tr")
+        nc.tensor.transpose(out=params_ps[:], in_=param_rows[:], identity=ident_bf16[:])
+        params = keep.tile([P, 3 * BLOCKS], F32)
+        nc.vector.tensor_copy(out=params[:], in_=params_ps[:, 0 : 3 * BLOCKS])
+
+        x_t = keep.tile([P, PASSES, HALVES, ROWS * 2], BF16)
+        pieces = ROWS * 2 // BN_MAX
+        stats0 = keep.tile([P, PASSES, HALVES, pieces, 6], F32)
+        moments0 = keep.tile([P, PASSES, PACK, 2], F32)
+        scale0 = keep.tile([P, PASSES, PACK], F32)
+        bias0 = keep.tile([P, PASSES, PACK], F32)
+        for g in range(PASSES):
+            for c in range(CHUNKS):
+                x_sb = xin.tile([P, ROW_TILES, K_PASS], BF16)
+                nc.sync.dma_start(
+                    out=x_sb[:], in_=x_view[c][:, :, g * K_PASS : (g + 1) * K_PASS]
+                )
+                for u in range(HALVES):
+                    x_ps = psum.tile([P, CHUNK], F32, tag="tr")
+                    for j in range(ROW_TILES):
+                        nc.tensor.transpose(
+                            out=x_ps[:, j * P : (j + 1) * P],
+                            in_=x_sb[:, j, :].bitcast(F32)[:, u : K_PASS // 2 : HALVES],
+                            identity=ident_f32[:],
+                        )
+                    lo = c * CHUNK * 2
+                    nc.scalar.copy(
+                        out=x_t[:, g, u, lo : lo + CHUNK * 2], in_=x_ps[:].bitcast(BF16)
+                    )
+                    for s in range(CHUNK * 2 // BN_MAX):
+                        piece = c * (CHUNK * 2 // BN_MAX) + s
+                        nc.vector.bn_stats(
+                            out=stats0[:, g, u, piece, :],
+                            in_=x_t[:, g, u, piece * BN_MAX : (piece + 1) * BN_MAX],
+                        )
+            for u in range(HALVES):
+                for e in range(2):
+                    nc.vector.bn_aggr(
+                        out=moments0[:, g, 2 * u + e, :],
+                        in_=stats0[:, g, u, :, 3 * e : 3 * e + 3],
+                    )
+            norm_coefficients(
+                nc,
+                small,
+                moments0[:, g, :, 0],
+                moments0[:, g, :, 1],
+                gain0[:, g, :],
+                shift0[:, g, :],
+                scale0[:, g, :],
+                bias0[:, g, :],
+                PACK,
+            )
+
+        w_codes = keep.tile([P, PASSES, D_OUT], U32, align_bytes=64)
+        for g in range(PASSES):
+            nc.sync.dma_start(
+                out=w_codes[:, g, :].bitcast(I32),
+                in_=W0_words[g].rearrange("p n t -> p (n t)").bitcast(I32),
+            )
+        for g in range(PASSES):
+            for q in range(4):
+                nc.sync.dma_start(
+                    out=w_scales[32 * q : 32 * q + 4, g, :].bitcast(I32),
+                    in_=W0_scales[g, 4 * q : 4 * q + 4, :].bitcast(I32),
+                )
+
+        x_codes = keep.tile([P, PASSES, ROWS], U32, align_bytes=64)
+        x_scales = keep.tile([P, PASSES, ROWS], U8, align_bytes=64)
+        for g in range(PASSES):
+            for c in range(CHUNKS):
+                cols = slice(c * CHUNK, (c + 1) * CHUNK)
+                planes = stage.tile([P, PACK, CHUNK], BF16)
+                for u in range(HALVES):
+                    pairs = x_t[:, g, u, :].rearrange("p (c e) -> p c e", e=2)
+                    for e in range(2):
+                        t = 2 * u + e
+                        nc.scalar.activation(
+                            out=planes[:, t, :],
+                            in_=pairs[:, cols, e],
+                            func=ACT.Identity,
+                            scale=scale0[:, g, t : t + 1],
+                            bias=bias0[:, g, t : t + 1],
+                        )
+                grouped = stage.tile([P, CHUNK, PACK], BF16, align_bytes=64)
+                nc.vector.tensor_copy(
+                    out=grouped[:].rearrange("p (c i) t -> p c t i", i=4),
+                    in_=planes[:].rearrange("p t (c i) -> p c t i", i=4),
+                )
+                nc.vector.quantize_mx(
+                    out=x_codes[:, g, cols].bitcast(FP8X4),
+                    scales=x_scales[:, g, cols],
+                    in_=grouped[:].rearrange("p c t -> p (c t)"),
+                )
+
+        def linear_block(b):
+            feats = slice(b * P, (b + 1) * P)
+            h = hidden.tile([P, ROWS], F32)
+            stats1 = small.tile([P, CHUNKS, 6], F32)
+            for c in range(CHUNKS):
+                cols = slice(c * CHUNK, (c + 1) * CHUNK)
+                acc = psum.tile([P, CHUNK], F32, tag="acc")
+                for g in range(PASSES):
+                    nc.tensor.matmul_mx(
+                        out=acc[:],
+                        lhsT=w_codes[:, g, feats].bitcast(FP8X4),
+                        lhsT_scale=w_scales[:, g, feats],
+                        rhs=x_codes[:, g, cols].bitcast(FP8X4),
+                        rhs_scale=x_scales[:, g, cols],
+                        start=(g == 0),
+                        stop=(g == PASSES - 1),
+                    )
+                nc.scalar.activation(
+                    out=h[:, cols], in_=acc[:], func=ACT.Relu, bias=params[:, b : b + 1]
+                )
+                nc.vector.bn_stats(out=stats1[:, c, :], in_=h[:, cols])
+            moments1 = small.tile([P, 2], F32)
+            nc.vector.bn_aggr(
+                out=moments1[:], in_=stats1[:].rearrange("p c (s v) -> p (c s) v", v=3)
+            )
+            scale1 = small.tile([P, 1], F32)
+            bias1 = small.tile([P, 1], F32)
+            norm_coefficients(
+                nc,
+                small,
+                moments1[:, 0:1],
+                moments1[:, 1:2],
+                params[:, BLOCKS + b : BLOCKS + b + 1],
+                params[:, 2 * BLOCKS + b : 2 * BLOCKS + b + 1],
+                scale1[:],
+                bias1[:],
+                1,
+            )
+            for c in range(0, CHUNKS, 2):
+                cols = slice(c * CHUNK, (c + 2) * CHUNK)
+                nc.gpsimd.tensor_scalar(
+                    out=h[:, cols],
+                    in0=h[:, cols],
+                    scalar1=scale1[:, 0:1],
+                    scalar2=bias1[:, 0:1],
+                    op0=ALU.mult,
+                    op1=ALU.add,
+                )
+            return h
+
+        def store_block(b, h):
+            for c in range(CHUNKS):
+                o_ps = psum.tile([P, ROW_TILES, P], F32, tag="tr")
+                for j in range(ROW_TILES):
+                    lo = c * CHUNK + j * P
+                    nc.tensor.transpose(
+                        out=o_ps[:, j, :], in_=h[:, lo : lo + P], identity=ident_f32[:]
+                    )
+                o_sb = outs.tile([P, ROW_TILES, P], F32)
+                if c % 2 == 0:
+                    nc.vector.tensor_copy(out=o_sb[:], in_=o_ps[:])
+                else:
+                    nc.scalar.copy(out=o_sb[:], in_=o_ps[:])
+                nc.sync.dma_start(
+                    out=out_view[c][:, :, b * P : (b + 1) * P], in_=o_sb[:]
+                )
+
+        waiting = None
+        for b in range(BLOCKS):
+            h = linear_block(b)
+            if waiting is not None:
+                store_block(b - 1, waiting)
+            waiting = h
+        store_block(BLOCKS - 1, waiting)

@@ -23,19 +23,23 @@ ROW_TILES = CHUNK // P
 BLOCKS = D_OUT // P
 HALVES = 2
 BN_MAX = 512
+AFFINE_COLS = 2048
+NORM_COLS = 1024
 EPS = 1e-5
 
 FLOPS = 2 * ROWS * D_IN * D_OUT
 
 
-def norm_coefficients(nc, pool, mean, var, gain, shift, scale_out, bias_out, width):
-    std = pool.tile([P, width], F32)
-    nc.vector.tensor_scalar_add(out=std[:], in0=var, scalar1=EPS)
-    nc.scalar.activation(out=std[:], in_=std[:], func=ACT.Sqrt)
-    nc.vector.reciprocal(out=std[:], in_=std[:])
-    nc.vector.tensor_mul(out=scale_out, in0=gain, in1=std[:])
-    nc.vector.tensor_mul(out=std[:], in0=mean, in1=scale_out)
-    nc.vector.tensor_sub(out=bias_out, in0=shift, in1=std[:])
+def norm_coefficients(nc, pool, neg_half, mean, var, gain, shift, scale_out, bias_out):
+    width = scale_out.shape[1]
+    rstd = pool.tile([P, width], F32)
+    nc.gpsimd.tensor_scalar(
+        out=rstd[:], in0=var, scalar1=1.0, scalar2=EPS, op0=ALU.mult, op1=ALU.add
+    )
+    nc.gpsimd.tensor_tensor(out=rstd[:], in0=rstd[:], in1=neg_half[:, 0:width], op=ALU.pow)
+    nc.gpsimd.tensor_mul(out=scale_out, in0=gain, in1=rstd[:])
+    nc.gpsimd.tensor_mul(out=rstd[:], in0=mean, in1=scale_out)
+    nc.gpsimd.tensor_sub(out=bias_out, in0=shift, in1=rstd[:])
 
 
 def tile_settransform_pa_t_kernel(
@@ -50,208 +54,214 @@ def tile_settransform_pa_t_kernel(
     )
 
     with tc.tile_pool(name="keep", bufs=1) as keep, tc.tile_pool(
-        name="xin", bufs=4
-    ) as xin, tc.tile_pool(name="stage", bufs=3) as stage, tc.tile_pool(
-        name="hidden", bufs=3
-    ) as hidden, tc.tile_pool(name="small", bufs=4) as small, tc.tile_pool(
-        name="outs", bufs=4
-    ) as outs, tc.psum_pool(name="psum", bufs=4) as psum:
-        warm = keep.tile([P, 1], F32)
-        nc.vector.memset(warm[:], 1.0)
-        nc.scalar.activation(out=warm[:], in_=warm[:], func=ACT.Sqrt)
-
+        name="small", bufs=4
+    ) as small, tc.psum_pool(name="psum", bufs=4) as psum, tc.manual_schedule():
         ident_f32 = keep.tile([P, P], F32)
         make_identity(nc, ident_f32[:])
         ident_bf16 = keep.tile([P, P], BF16)
         make_identity(nc, ident_bf16[:])
+        neg_half = keep.tile([P, PACK], F32)
+        nc.gpsimd.memset(neg_half[:], -0.5)
 
         w_scales = keep.tile([P, PASSES, D_OUT], U8, align_bytes=64)
         nc.vector.memset(w_scales[:].rearrange("p g n -> p (g n)").bitcast(I32), 0)
         param_rows = keep.tile([P, P], BF16)
         nc.vector.memset(param_rows[:], 0.0)
 
-        gain0_bf = keep.tile([P, PASSES, PACK], BF16)
-        shift0_bf = keep.tile([P, PASSES, PACK], BF16)
-        nc.scalar.dma_start(
-            out=gain0_bf[:], in_=g0.rearrange("(g p t) -> p g t", g=PASSES, p=P)
-        )
-        nc.scalar.dma_start(
-            out=shift0_bf[:], in_=b0.rearrange("(g p t) -> p g t", g=PASSES, p=P)
-        )
+        gain0 = keep.tile([P, PASSES, PACK], BF16)
+        shift0 = keep.tile([P, PASSES, PACK], BF16)
+        nc.scalar.dma_start(out=gain0[:], in_=g0.rearrange("(g p t) -> p g t", g=PASSES, p=P))
+        nc.scalar.dma_start(out=shift0[:], in_=b0.rearrange("(g p t) -> p g t", g=PASSES, p=P))
         for v, vec in enumerate((c0, g1, b1)):
             nc.scalar.dma_start(
                 out=param_rows[v * BLOCKS : (v + 1) * BLOCKS, :],
                 in_=vec.rearrange("(b p) -> b p", p=P),
             )
-        gain0 = keep.tile([P, PASSES, PACK], F32)
-        shift0 = keep.tile([P, PASSES, PACK], F32)
-        nc.vector.tensor_copy(out=gain0[:], in_=gain0_bf[:])
-        nc.vector.tensor_copy(out=shift0[:], in_=shift0_bf[:])
-        params_ps = psum.tile([P, P], BF16, tag="tr")
-        nc.tensor.transpose(out=params_ps[:], in_=param_rows[:], identity=ident_bf16[:])
-        params = keep.tile([P, 3 * BLOCKS], F32)
-        nc.vector.tensor_copy(out=params[:], in_=params_ps[:, 0 : 3 * BLOCKS])
-
-        x_t = keep.tile([P, PASSES, HALVES, ROWS * 2], BF16)
-        pieces = ROWS * 2 // BN_MAX
-        stats0 = keep.tile([P, PASSES, HALVES, pieces, 6], F32)
-        moments0 = keep.tile([P, PASSES, PACK, 2], F32)
-        scale0 = keep.tile([P, PASSES, PACK], F32)
-        bias0 = keep.tile([P, PASSES, PACK], F32)
-        for g in range(PASSES):
-            for c in range(CHUNKS):
-                x_sb = xin.tile([P, ROW_TILES, K_PASS], BF16)
-                nc.sync.dma_start(
-                    out=x_sb[:], in_=x_view[c][:, :, g * K_PASS : (g + 1) * K_PASS]
-                )
-                for u in range(HALVES):
-                    x_ps = psum.tile([P, CHUNK], F32, tag="tr")
-                    for j in range(ROW_TILES):
-                        nc.tensor.transpose(
-                            out=x_ps[:, j * P : (j + 1) * P],
-                            in_=x_sb[:, j, :].bitcast(F32)[:, u : K_PASS // 2 : HALVES],
-                            identity=ident_f32[:],
-                        )
-                    lo = c * CHUNK * 2
-                    nc.scalar.copy(
-                        out=x_t[:, g, u, lo : lo + CHUNK * 2], in_=x_ps[:].bitcast(BF16)
-                    )
-                    for s in range(CHUNK * 2 // BN_MAX):
-                        piece = c * (CHUNK * 2 // BN_MAX) + s
-                        nc.vector.bn_stats(
-                            out=stats0[:, g, u, piece, :],
-                            in_=x_t[:, g, u, piece * BN_MAX : (piece + 1) * BN_MAX],
-                        )
-            for u in range(HALVES):
-                for e in range(2):
-                    nc.vector.bn_aggr(
-                        out=moments0[:, g, 2 * u + e, :],
-                        in_=stats0[:, g, u, :, 3 * e : 3 * e + 3],
-                    )
-            norm_coefficients(
-                nc,
-                small,
-                moments0[:, g, :, 0],
-                moments0[:, g, :, 1],
-                gain0[:, g, :],
-                shift0[:, g, :],
-                scale0[:, g, :],
-                bias0[:, g, :],
-                PACK,
-            )
 
         w_codes = keep.tile([P, PASSES, D_OUT], U32, align_bytes=64)
-        for g in range(PASSES):
-            nc.sync.dma_start(
-                out=w_codes[:, g, :].bitcast(I32),
-                in_=W0_words[g].rearrange("p n t -> p (n t)").bitcast(I32),
-            )
-        for g in range(PASSES):
-            for q in range(4):
-                nc.sync.dma_start(
-                    out=w_scales[32 * q : 32 * q + 4, g, :].bitcast(I32),
-                    in_=W0_scales[g, 4 * q : 4 * q + 4, :].bitcast(I32),
-                )
-
         x_codes = keep.tile([P, PASSES, ROWS], U32, align_bytes=64)
         x_scales = keep.tile([P, PASSES, ROWS], U8, align_bytes=64)
-        for g in range(PASSES):
-            for c in range(CHUNKS):
-                cols = slice(c * CHUNK, (c + 1) * CHUNK)
-                planes = stage.tile([P, PACK, CHUNK], BF16)
-                for u in range(HALVES):
-                    pairs = x_t[:, g, u, :].rearrange("p (c e) -> p c e", e=2)
-                    for e in range(2):
-                        t = 2 * u + e
-                        nc.scalar.activation(
-                            out=planes[:, t, :],
-                            in_=pairs[:, cols, e],
-                            func=ACT.Identity,
-                            scale=scale0[:, g, t : t + 1],
-                            bias=bias0[:, g, t : t + 1],
-                        )
-                grouped = stage.tile([P, CHUNK, PACK], BF16, align_bytes=64)
-                nc.vector.tensor_copy(
-                    out=grouped[:].rearrange("p (c i) t -> p c t i", i=4),
-                    in_=planes[:].rearrange("p t (c i) -> p c t i", i=4),
-                )
-                nc.vector.quantize_mx(
-                    out=x_codes[:, g, cols].bitcast(FP8X4),
-                    scales=x_scales[:, g, cols],
-                    in_=grouped[:].rearrange("p c t -> p (c t)"),
-                )
+        params = keep.tile([P, 3 * BLOCKS], F32)
 
-        def linear_block(b):
-            feats = slice(b * P, (b + 1) * P)
-            h = hidden.tile([P, ROWS], F32)
-            stats1 = small.tile([P, CHUNKS, 6], F32)
-            for c in range(CHUNKS):
-                cols = slice(c * CHUNK, (c + 1) * CHUNK)
-                acc = psum.tile([P, CHUNK], F32, tag="acc")
+        with tc.tile_pool(name="early", bufs=1) as early:
+            x_t = early.tile([P, PASSES, HALVES, ROWS * 2], BF16)
+            pieces = ROWS * 2 // BN_MAX
+            stats0 = early.tile([P, PASSES, HALVES, pieces, 6], F32)
+            moments0 = early.tile([P, PASSES, PACK, 2], F32)
+            scale0 = early.tile([P, PASSES, PACK], F32)
+            bias0 = early.tile([P, PASSES, PACK], F32)
+
+            with tc.tile_pool(name="xin", bufs=8) as xin:
                 for g in range(PASSES):
-                    nc.tensor.matmul_mx(
-                        out=acc[:],
-                        lhsT=w_codes[:, g, feats].bitcast(FP8X4),
-                        lhsT_scale=w_scales[:, g, feats],
-                        rhs=x_codes[:, g, cols].bitcast(FP8X4),
-                        rhs_scale=x_scales[:, g, cols],
-                        start=(g == 0),
-                        stop=(g == PASSES - 1),
+                    for c in range(CHUNKS):
+                        x_sb = xin.tile([P, ROW_TILES, K_PASS], BF16)
+                        nc.sync.dma_start(
+                            out=x_sb[:], in_=x_view[c][:, :, g * K_PASS : (g + 1) * K_PASS]
+                        )
+                        for u in range(HALVES):
+                            x_ps = psum.tile([P, CHUNK], F32, tag="tr")
+                            for j in range(ROW_TILES):
+                                nc.tensor.transpose(
+                                    out=x_ps[:, j * P : (j + 1) * P],
+                                    in_=x_sb[:, j, :].bitcast(F32)[:, u : K_PASS // 2 : HALVES],
+                                    identity=ident_f32[:],
+                                )
+                            lo = c * CHUNK * 2
+                            nc.scalar.copy(
+                                out=x_t[:, g, u, lo : lo + CHUNK * 2],
+                                in_=x_ps[:].bitcast(BF16),
+                            )
+                            for s in range(CHUNK * 2 // BN_MAX):
+                                piece = c * (CHUNK * 2 // BN_MAX) + s
+                                nc.vector.bn_stats(
+                                    out=stats0[:, g, u, piece, :],
+                                    in_=x_t[:, g, u, piece * BN_MAX : (piece + 1) * BN_MAX],
+                                )
+                    for u in range(HALVES):
+                        for e in range(2):
+                            nc.vector.bn_aggr(
+                                out=moments0[:, g, 2 * u + e, :],
+                                in_=stats0[:, g, u, :, 3 * e : 3 * e + 3],
+                            )
+                    norm_coefficients(
+                        nc,
+                        small,
+                        neg_half,
+                        moments0[:, g, :, 0],
+                        moments0[:, g, :, 1],
+                        gain0[:, g, :],
+                        shift0[:, g, :],
+                        scale0[:, g, :],
+                        bias0[:, g, :],
                     )
-                nc.scalar.activation(
-                    out=h[:, cols], in_=acc[:], func=ACT.Relu, bias=params[:, b : b + 1]
-                )
-                nc.vector.bn_stats(out=stats1[:, c, :], in_=h[:, cols])
-            moments1 = small.tile([P, 2], F32)
-            nc.vector.bn_aggr(
-                out=moments1[:], in_=stats1[:].rearrange("p c (s v) -> p (c s) v", v=3)
-            )
-            scale1 = small.tile([P, 1], F32)
-            bias1 = small.tile([P, 1], F32)
-            norm_coefficients(
-                nc,
-                small,
-                moments1[:, 0:1],
-                moments1[:, 1:2],
-                params[:, BLOCKS + b : BLOCKS + b + 1],
-                params[:, 2 * BLOCKS + b : 2 * BLOCKS + b + 1],
-                scale1[:],
-                bias1[:],
-                1,
-            )
-            for c in range(0, CHUNKS, 2):
-                cols = slice(c * CHUNK, (c + 2) * CHUNK)
-                nc.gpsimd.tensor_scalar(
-                    out=h[:, cols],
-                    in0=h[:, cols],
-                    scalar1=scale1[:, 0:1],
-                    scalar2=bias1[:, 0:1],
-                    op0=ALU.mult,
-                    op1=ALU.add,
-                )
-            return h
 
-        def store_block(b, h):
-            for c in range(CHUNKS):
-                o_ps = psum.tile([P, ROW_TILES, P], F32, tag="tr")
-                for j in range(ROW_TILES):
-                    lo = c * CHUNK + j * P
-                    nc.tensor.transpose(
-                        out=o_ps[:, j, :], in_=h[:, lo : lo + P], identity=ident_f32[:]
-                    )
-                o_sb = outs.tile([P, ROW_TILES, P], F32)
-                if c % 2 == 0:
-                    nc.vector.tensor_copy(out=o_sb[:], in_=o_ps[:])
-                else:
-                    nc.scalar.copy(out=o_sb[:], in_=o_ps[:])
+            for g in range(PASSES):
                 nc.sync.dma_start(
-                    out=out_view[c][:, :, b * P : (b + 1) * P], in_=o_sb[:]
+                    out=w_codes[:, g, :].bitcast(I32),
+                    in_=W0_words[g].rearrange("p n t -> p (n t)").bitcast(I32),
                 )
+            for g in range(PASSES):
+                for q in range(4):
+                    nc.sync.dma_start(
+                        out=w_scales[32 * q : 32 * q + 4, g, :].bitcast(I32),
+                        in_=W0_scales[g, 4 * q : 4 * q + 4, :].bitcast(I32),
+                    )
+            params_ps = psum.tile([P, P], BF16, tag="tr")
+            nc.tensor.transpose(out=params_ps[:], in_=param_rows[:], identity=ident_bf16[:])
+            nc.vector.tensor_copy(out=params[:], in_=params_ps[:, 0 : 3 * BLOCKS])
 
-        waiting = None
-        for b in range(BLOCKS):
-            h = linear_block(b)
-            if waiting is not None:
-                store_block(b - 1, waiting)
-            waiting = h
-        store_block(BLOCKS - 1, waiting)
+            with tc.tile_pool(name="stage", bufs=2) as stage, tc.tile_pool(
+                name="words", bufs=3
+            ) as words:
+
+                def quantise(g, cols, grouped):
+                    nc.vector.quantize_mx(
+                        out=x_codes[:, g, cols].bitcast(FP8X4),
+                        scales=x_scales[:, g, cols],
+                        in_=grouped[:].rearrange("p c t -> p (c t)"),
+                    )
+
+                waiting = None
+                for g in range(PASSES):
+                    for a in range(ROWS // AFFINE_COLS):
+                        planes = stage.tile([P, PACK, AFFINE_COLS], BF16)
+                        for u in range(HALVES):
+                            pairs = x_t[:, g, u, :].rearrange("p (c e) -> p c e", e=2)
+                            for e in range(2):
+                                t = 2 * u + e
+                                nc.scalar.activation(
+                                    out=planes[:, t, :],
+                                    in_=pairs[:, a * AFFINE_COLS : (a + 1) * AFFINE_COLS, e],
+                                    func=ACT.Identity,
+                                    scale=scale0[:, g, t : t + 1],
+                                    bias=bias0[:, g, t : t + 1],
+                                )
+                        for s in range(AFFINE_COLS // CHUNK):
+                            grouped = words.tile([P, CHUNK, PACK], BF16, align_bytes=64)
+                            nc.vector.tensor_copy(
+                                out=grouped[:].rearrange("p (c i) t -> p c t i", i=4),
+                                in_=planes[:, :, s * CHUNK : (s + 1) * CHUNK].rearrange(
+                                    "p t (c i) -> p c t i", i=4
+                                ),
+                            )
+                            if waiting is not None:
+                                quantise(*waiting)
+                            lo = a * AFFINE_COLS + s * CHUNK
+                            waiting = (g, slice(lo, lo + CHUNK), grouped)
+                quantise(*waiting)
+
+        with tc.tile_pool(name="hidden", bufs=3) as hidden, tc.tile_pool(
+            name="outs", bufs=8
+        ) as outs:
+
+            def linear_block(b):
+                feats = slice(b * P, (b + 1) * P)
+                h = hidden.tile([P, ROWS], F32)
+                stats1 = small.tile([P, CHUNKS, 6], F32)
+                for c in range(CHUNKS):
+                    cols = slice(c * CHUNK, (c + 1) * CHUNK)
+                    acc = psum.tile([P, CHUNK], F32, tag="acc")
+                    for g in range(PASSES):
+                        nc.tensor.matmul_mx(
+                            out=acc[:],
+                            lhsT=w_codes[:, g, feats].bitcast(FP8X4),
+                            lhsT_scale=w_scales[:, g, feats],
+                            rhs=x_codes[:, g, cols].bitcast(FP8X4),
+                            rhs_scale=x_scales[:, g, cols],
+                            start=(g == 0),
+                            stop=(g == PASSES - 1),
+                        )
+                    nc.scalar.activation(
+                        out=h[:, cols], in_=acc[:], func=ACT.Relu, bias=params[:, b : b + 1]
+                    )
+                    nc.vector.bn_stats(out=stats1[:, c, :], in_=h[:, cols])
+                moments1 = small.tile([P, 2], F32)
+                nc.vector.bn_aggr(
+                    out=moments1[:], in_=stats1[:].rearrange("p c (s v) -> p (c s) v", v=3)
+                )
+                scale1 = small.tile([P, 1], F32)
+                bias1 = small.tile([P, 1], F32)
+                norm_coefficients(
+                    nc,
+                    small,
+                    neg_half,
+                    moments1[:, 0:1],
+                    moments1[:, 1:2],
+                    params[:, BLOCKS + b : BLOCKS + b + 1],
+                    params[:, 2 * BLOCKS + b : 2 * BLOCKS + b + 1],
+                    scale1[:],
+                    bias1[:],
+                )
+                for lo in range(0, ROWS, NORM_COLS):
+                    nc.gpsimd.tensor_scalar(
+                        out=h[:, lo : lo + NORM_COLS],
+                        in0=h[:, lo : lo + NORM_COLS],
+                        scalar1=scale1[:, 0:1],
+                        scalar2=bias1[:, 0:1],
+                        op0=ALU.mult,
+                        op1=ALU.add,
+                    )
+                return h
+
+            def store_block(b, h):
+                for c in range(CHUNKS):
+                    o_ps = psum.tile([P, ROW_TILES, P], F32, tag="tr")
+                    for j in range(ROW_TILES):
+                        lo = c * CHUNK + j * P
+                        nc.tensor.transpose(
+                            out=o_ps[:, j, :], in_=h[:, lo : lo + P], identity=ident_f32[:]
+                        )
+                    o_sb = outs.tile([P, ROW_TILES, P], F32)
+                    if c % 2 == 0:
+                        nc.vector.tensor_copy(out=o_sb[:], in_=o_ps[:])
+                    else:
+                        nc.scalar.copy(out=o_sb[:], in_=o_ps[:])
+                    nc.sync.dma_start(out=out_view[c][:, :, b * P : (b + 1) * P], in_=o_sb[:])
+
+            previous = None
+            for b in range(BLOCKS):
+                h = linear_block(b)
+                if previous is not None:
+                    store_block(b - 1, previous)
+                previous = h
+            store_block(BLOCKS - 1, previous)

@@ -23,23 +23,19 @@ ROW_TILES = CHUNK // P
 BLOCKS = D_OUT // P
 HALVES = 2
 BN_MAX = 512
-AFFINE_COLS = 2048
-NORM_COLS = 1024
 EPS = 1e-5
 
 FLOPS = 2 * ROWS * D_IN * D_OUT
 
 
-def norm_coefficients(nc, pool, neg_half, mean, var, gain, shift, scale_out, bias_out):
-    width = scale_out.shape[1]
-    rstd = pool.tile([P, width], F32)
-    nc.gpsimd.tensor_scalar(
-        out=rstd[:], in0=var, scalar1=1.0, scalar2=EPS, op0=ALU.mult, op1=ALU.add
-    )
-    nc.gpsimd.tensor_tensor(out=rstd[:], in0=rstd[:], in1=neg_half[:, 0:width], op=ALU.pow)
-    nc.gpsimd.tensor_mul(out=scale_out, in0=gain, in1=rstd[:])
-    nc.gpsimd.tensor_mul(out=rstd[:], in0=mean, in1=scale_out)
-    nc.gpsimd.tensor_sub(out=bias_out, in0=shift, in1=rstd[:])
+def norm_coefficients(nc, pool, mean, var, gain, shift, scale_out, bias_out, width):
+    std = pool.tile([P, width], F32)
+    nc.vector.tensor_scalar_add(out=std[:], in0=var, scalar1=EPS)
+    nc.scalar.activation(out=std[:], in_=std[:], func=ACT.Sqrt)
+    nc.vector.reciprocal(out=std[:], in_=std[:])
+    nc.vector.tensor_mul(out=scale_out, in0=gain, in1=std[:])
+    nc.vector.tensor_mul(out=std[:], in0=mean, in1=scale_out)
+    nc.vector.tensor_sub(out=bias_out, in0=shift, in1=std[:])
 
 
 def tile_settransform_pa_t_kernel(
@@ -54,214 +50,208 @@ def tile_settransform_pa_t_kernel(
     )
 
     with tc.tile_pool(name="keep", bufs=1) as keep, tc.tile_pool(
-        name="small", bufs=4
-    ) as small, tc.psum_pool(name="psum", bufs=4) as psum, tc.manual_schedule():
+        name="xin", bufs=4
+    ) as xin, tc.tile_pool(name="stage", bufs=3) as stage, tc.tile_pool(
+        name="hidden", bufs=3
+    ) as hidden, tc.tile_pool(name="small", bufs=4) as small, tc.tile_pool(
+        name="outs", bufs=4
+    ) as outs, tc.psum_pool(name="psum", bufs=4) as psum:
+        warm = keep.tile([P, 1], F32)
+        nc.vector.memset(warm[:], 1.0)
+        nc.scalar.activation(out=warm[:], in_=warm[:], func=ACT.Sqrt)
+
         ident_f32 = keep.tile([P, P], F32)
         make_identity(nc, ident_f32[:])
         ident_bf16 = keep.tile([P, P], BF16)
         make_identity(nc, ident_bf16[:])
-        neg_half = keep.tile([P, PACK], F32)
-        nc.gpsimd.memset(neg_half[:], -0.5)
 
         w_scales = keep.tile([P, PASSES, D_OUT], U8, align_bytes=64)
         nc.vector.memset(w_scales[:].rearrange("p g n -> p (g n)").bitcast(I32), 0)
         param_rows = keep.tile([P, P], BF16)
         nc.vector.memset(param_rows[:], 0.0)
 
-        gain0 = keep.tile([P, PASSES, PACK], BF16)
-        shift0 = keep.tile([P, PASSES, PACK], BF16)
-        nc.scalar.dma_start(out=gain0[:], in_=g0.rearrange("(g p t) -> p g t", g=PASSES, p=P))
-        nc.scalar.dma_start(out=shift0[:], in_=b0.rearrange("(g p t) -> p g t", g=PASSES, p=P))
+        gain0_bf = keep.tile([P, PASSES, PACK], BF16)
+        shift0_bf = keep.tile([P, PASSES, PACK], BF16)
+        nc.scalar.dma_start(
+            out=gain0_bf[:], in_=g0.rearrange("(g p t) -> p g t", g=PASSES, p=P)
+        )
+        nc.scalar.dma_start(
+            out=shift0_bf[:], in_=b0.rearrange("(g p t) -> p g t", g=PASSES, p=P)
+        )
         for v, vec in enumerate((c0, g1, b1)):
             nc.scalar.dma_start(
                 out=param_rows[v * BLOCKS : (v + 1) * BLOCKS, :],
                 in_=vec.rearrange("(b p) -> b p", p=P),
             )
+        gain0 = keep.tile([P, PASSES, PACK], F32)
+        shift0 = keep.tile([P, PASSES, PACK], F32)
+        nc.vector.tensor_copy(out=gain0[:], in_=gain0_bf[:])
+        nc.vector.tensor_copy(out=shift0[:], in_=shift0_bf[:])
+        params_ps = psum.tile([P, P], BF16, tag="tr")
+        nc.tensor.transpose(out=params_ps[:], in_=param_rows[:], identity=ident_bf16[:])
+        params = keep.tile([P, 3 * BLOCKS], F32)
+        nc.vector.tensor_copy(out=params[:], in_=params_ps[:, 0 : 3 * BLOCKS])
+
+        x_t = keep.tile([P, PASSES, HALVES, ROWS * 2], BF16)
+        pieces = ROWS * 2 // BN_MAX
+        stats0 = keep.tile([P, PASSES, HALVES, pieces, 6], F32)
+        moments0 = keep.tile([P, PASSES, PACK, 2], F32)
+        scale0 = keep.tile([P, PASSES, PACK], F32)
+        bias0 = keep.tile([P, PASSES, PACK], F32)
+        for g in range(PASSES):
+            for c in range(CHUNKS):
+                x_sb = xin.tile([P, ROW_TILES, K_PASS], BF16)
+                nc.sync.dma_start(
+                    out=x_sb[:], in_=x_view[c][:, :, g * K_PASS : (g + 1) * K_PASS]
+                )
+                for u in range(HALVES):
+                    x_ps = psum.tile([P, CHUNK], F32, tag="tr")
+                    for j in range(ROW_TILES):
+                        nc.tensor.transpose(
+                            out=x_ps[:, j * P : (j + 1) * P],
+                            in_=x_sb[:, j, :].bitcast(F32)[:, u : K_PASS // 2 : HALVES],
+                            identity=ident_f32[:],
+                        )
+                    lo = c * CHUNK * 2
+                    nc.scalar.copy(
+                        out=x_t[:, g, u, lo : lo + CHUNK * 2], in_=x_ps[:].bitcast(BF16)
+                    )
+                    for s in range(CHUNK * 2 // BN_MAX):
+                        piece = c * (CHUNK * 2 // BN_MAX) + s
+                        nc.vector.bn_stats(
+                            out=stats0[:, g, u, piece, :],
+                            in_=x_t[:, g, u, piece * BN_MAX : (piece + 1) * BN_MAX],
+                        )
+            for u in range(HALVES):
+                for e in range(2):
+                    nc.vector.bn_aggr(
+                        out=moments0[:, g, 2 * u + e, :],
+                        in_=stats0[:, g, u, :, 3 * e : 3 * e + 3],
+                    )
+            norm_coefficients(
+                nc,
+                small,
+                moments0[:, g, :, 0],
+                moments0[:, g, :, 1],
+                gain0[:, g, :],
+                shift0[:, g, :],
+                scale0[:, g, :],
+                bias0[:, g, :],
+                PACK,
+            )
 
         w_codes = keep.tile([P, PASSES, D_OUT], U32, align_bytes=64)
+        for g in range(PASSES):
+            nc.sync.dma_start(
+                out=w_codes[:, g, :].bitcast(I32),
+                in_=W0_words[g].rearrange("p n t -> p (n t)").bitcast(I32),
+            )
+        for g in range(PASSES):
+            for q in range(4):
+                nc.sync.dma_start(
+                    out=w_scales[32 * q : 32 * q + 4, g, :].bitcast(I32),
+                    in_=W0_scales[g, 4 * q : 4 * q + 4, :].bitcast(I32),
+                )
+
         x_codes = keep.tile([P, PASSES, ROWS], U32, align_bytes=64)
         x_scales = keep.tile([P, PASSES, ROWS], U8, align_bytes=64)
-        params = keep.tile([P, 3 * BLOCKS], F32)
-
-        with tc.tile_pool(name="early", bufs=1) as early:
-            x_t = early.tile([P, PASSES, HALVES, ROWS * 2], BF16)
-            pieces = ROWS * 2 // BN_MAX
-            stats0 = early.tile([P, PASSES, HALVES, pieces, 6], F32)
-            moments0 = early.tile([P, PASSES, PACK, 2], F32)
-            scale0 = early.tile([P, PASSES, PACK], F32)
-            bias0 = early.tile([P, PASSES, PACK], F32)
-
-            with tc.tile_pool(name="xin", bufs=8) as xin:
-                for g in range(PASSES):
-                    for c in range(CHUNKS):
-                        x_sb = xin.tile([P, ROW_TILES, K_PASS], BF16)
-                        nc.sync.dma_start(
-                            out=x_sb[:], in_=x_view[c][:, :, g * K_PASS : (g + 1) * K_PASS]
+        for g in range(PASSES):
+            for c in range(CHUNKS):
+                cols = slice(c * CHUNK, (c + 1) * CHUNK)
+                planes = stage.tile([P, PACK, CHUNK], BF16)
+                for u in range(HALVES):
+                    pairs = x_t[:, g, u, :].rearrange("p (c e) -> p c e", e=2)
+                    for e in range(2):
+                        t = 2 * u + e
+                        nc.scalar.activation(
+                            out=planes[:, t, :],
+                            in_=pairs[:, cols, e],
+                            func=ACT.Identity,
+                            scale=scale0[:, g, t : t + 1],
+                            bias=bias0[:, g, t : t + 1],
                         )
-                        for u in range(HALVES):
-                            x_ps = psum.tile([P, CHUNK], F32, tag="tr")
-                            for j in range(ROW_TILES):
-                                nc.tensor.transpose(
-                                    out=x_ps[:, j * P : (j + 1) * P],
-                                    in_=x_sb[:, j, :].bitcast(F32)[:, u : K_PASS // 2 : HALVES],
-                                    identity=ident_f32[:],
-                                )
-                            lo = c * CHUNK * 2
-                            nc.scalar.copy(
-                                out=x_t[:, g, u, lo : lo + CHUNK * 2],
-                                in_=x_ps[:].bitcast(BF16),
-                            )
-                            for s in range(CHUNK * 2 // BN_MAX):
-                                piece = c * (CHUNK * 2 // BN_MAX) + s
-                                nc.vector.bn_stats(
-                                    out=stats0[:, g, u, piece, :],
-                                    in_=x_t[:, g, u, piece * BN_MAX : (piece + 1) * BN_MAX],
-                                )
-                    for u in range(HALVES):
-                        for e in range(2):
-                            nc.vector.bn_aggr(
-                                out=moments0[:, g, 2 * u + e, :],
-                                in_=stats0[:, g, u, :, 3 * e : 3 * e + 3],
-                            )
-                    norm_coefficients(
-                        nc,
-                        small,
-                        neg_half,
-                        moments0[:, g, :, 0],
-                        moments0[:, g, :, 1],
-                        gain0[:, g, :],
-                        shift0[:, g, :],
-                        scale0[:, g, :],
-                        bias0[:, g, :],
-                    )
+                grouped = stage.tile([P, CHUNK, PACK], BF16, align_bytes=64)
+                nc.vector.tensor_copy(
+                    out=grouped[:].rearrange("p (c i) t -> p c t i", i=4),
+                    in_=planes[:].rearrange("p t (c i) -> p c t i", i=4),
+                )
+                nc.vector.quantize_mx(
+                    out=x_codes[:, g, cols].bitcast(FP8X4),
+                    scales=x_scales[:, g, cols],
+                    in_=grouped[:].rearrange("p c t -> p (c t)"),
+                )
 
-            for g in range(PASSES):
+        def linear_block(b):
+            feats = slice(b * P, (b + 1) * P)
+            h = hidden.tile([P, ROWS], F32)
+            stats1 = small.tile([P, CHUNKS, 6], F32)
+            for c in range(CHUNKS):
+                cols = slice(c * CHUNK, (c + 1) * CHUNK)
+                acc = psum.tile([P, CHUNK], F32, tag="acc")
+                for g in range(PASSES):
+                    nc.tensor.matmul_mx(
+                        out=acc[:],
+                        lhsT=w_codes[:, g, feats].bitcast(FP8X4),
+                        lhsT_scale=w_scales[:, g, feats],
+                        rhs=x_codes[:, g, cols].bitcast(FP8X4),
+                        rhs_scale=x_scales[:, g, cols],
+                        start=(g == 0),
+                        stop=(g == PASSES - 1),
+                    )
+                nc.scalar.activation(
+                    out=h[:, cols], in_=acc[:], func=ACT.Relu, bias=params[:, b : b + 1]
+                )
+                nc.vector.bn_stats(out=stats1[:, c, :], in_=h[:, cols])
+            moments1 = small.tile([P, 2], F32)
+            nc.vector.bn_aggr(
+                out=moments1[:], in_=stats1[:].rearrange("p c (s v) -> p (c s) v", v=3)
+            )
+            scale1 = small.tile([P, 1], F32)
+            bias1 = small.tile([P, 1], F32)
+            norm_coefficients(
+                nc,
+                small,
+                moments1[:, 0:1],
+                moments1[:, 1:2],
+                params[:, BLOCKS + b : BLOCKS + b + 1],
+                params[:, 2 * BLOCKS + b : 2 * BLOCKS + b + 1],
+                scale1[:],
+                bias1[:],
+                1,
+            )
+            for c in range(0, CHUNKS, 2):
+                cols = slice(c * CHUNK, (c + 2) * CHUNK)
+                nc.vector.tensor_scalar(
+                    out=h[:, cols],
+                    in0=h[:, cols],
+                    scalar1=scale1[:, 0:1],
+                    scalar2=bias1[:, 0:1],
+                    op0=ALU.mult,
+                    op1=ALU.add,
+                )
+            return h
+
+        def store_block(b, h):
+            for c in range(CHUNKS):
+                o_ps = psum.tile([P, ROW_TILES, P], F32, tag="tr")
+                for j in range(ROW_TILES):
+                    lo = c * CHUNK + j * P
+                    nc.tensor.transpose(
+                        out=o_ps[:, j, :], in_=h[:, lo : lo + P], identity=ident_f32[:]
+                    )
+                o_sb = outs.tile([P, ROW_TILES, P], F32)
+                if c % 2 == 0:
+                    nc.vector.tensor_copy(out=o_sb[:], in_=o_ps[:])
+                else:
+                    nc.scalar.copy(out=o_sb[:], in_=o_ps[:])
                 nc.sync.dma_start(
-                    out=w_codes[:, g, :].bitcast(I32),
-                    in_=W0_words[g].rearrange("p n t -> p (n t)").bitcast(I32),
+                    out=out_view[c][:, :, b * P : (b + 1) * P], in_=o_sb[:]
                 )
-            for g in range(PASSES):
-                for q in range(4):
-                    nc.sync.dma_start(
-                        out=w_scales[32 * q : 32 * q + 4, g, :].bitcast(I32),
-                        in_=W0_scales[g, 4 * q : 4 * q + 4, :].bitcast(I32),
-                    )
-            params_ps = psum.tile([P, P], BF16, tag="tr")
-            nc.tensor.transpose(out=params_ps[:], in_=param_rows[:], identity=ident_bf16[:])
-            nc.vector.tensor_copy(out=params[:], in_=params_ps[:, 0 : 3 * BLOCKS])
 
-            with tc.tile_pool(name="stage", bufs=2) as stage, tc.tile_pool(
-                name="words", bufs=3
-            ) as words:
-
-                def quantise(g, cols, grouped):
-                    nc.vector.quantize_mx(
-                        out=x_codes[:, g, cols].bitcast(FP8X4),
-                        scales=x_scales[:, g, cols],
-                        in_=grouped[:].rearrange("p c t -> p (c t)"),
-                    )
-
-                waiting = None
-                for g in range(PASSES):
-                    for a in range(ROWS // AFFINE_COLS):
-                        planes = stage.tile([P, PACK, AFFINE_COLS], BF16)
-                        for u in range(HALVES):
-                            pairs = x_t[:, g, u, :].rearrange("p (c e) -> p c e", e=2)
-                            for e in range(2):
-                                t = 2 * u + e
-                                nc.scalar.activation(
-                                    out=planes[:, t, :],
-                                    in_=pairs[:, a * AFFINE_COLS : (a + 1) * AFFINE_COLS, e],
-                                    func=ACT.Identity,
-                                    scale=scale0[:, g, t : t + 1],
-                                    bias=bias0[:, g, t : t + 1],
-                                )
-                        for s in range(AFFINE_COLS // CHUNK):
-                            grouped = words.tile([P, CHUNK, PACK], BF16, align_bytes=64)
-                            nc.vector.tensor_copy(
-                                out=grouped[:].rearrange("p (c i) t -> p c t i", i=4),
-                                in_=planes[:, :, s * CHUNK : (s + 1) * CHUNK].rearrange(
-                                    "p t (c i) -> p c t i", i=4
-                                ),
-                            )
-                            if waiting is not None:
-                                quantise(*waiting)
-                            lo = a * AFFINE_COLS + s * CHUNK
-                            waiting = (g, slice(lo, lo + CHUNK), grouped)
-                quantise(*waiting)
-
-        with tc.tile_pool(name="hidden", bufs=3) as hidden, tc.tile_pool(
-            name="outs", bufs=8
-        ) as outs:
-
-            def linear_block(b):
-                feats = slice(b * P, (b + 1) * P)
-                h = hidden.tile([P, ROWS], F32)
-                stats1 = small.tile([P, CHUNKS, 6], F32)
-                for c in range(CHUNKS):
-                    cols = slice(c * CHUNK, (c + 1) * CHUNK)
-                    acc = psum.tile([P, CHUNK], F32, tag="acc")
-                    for g in range(PASSES):
-                        nc.tensor.matmul_mx(
-                            out=acc[:],
-                            lhsT=w_codes[:, g, feats].bitcast(FP8X4),
-                            lhsT_scale=w_scales[:, g, feats],
-                            rhs=x_codes[:, g, cols].bitcast(FP8X4),
-                            rhs_scale=x_scales[:, g, cols],
-                            start=(g == 0),
-                            stop=(g == PASSES - 1),
-                        )
-                    nc.scalar.activation(
-                        out=h[:, cols], in_=acc[:], func=ACT.Relu, bias=params[:, b : b + 1]
-                    )
-                    nc.vector.bn_stats(out=stats1[:, c, :], in_=h[:, cols])
-                moments1 = small.tile([P, 2], F32)
-                nc.vector.bn_aggr(
-                    out=moments1[:], in_=stats1[:].rearrange("p c (s v) -> p (c s) v", v=3)
-                )
-                scale1 = small.tile([P, 1], F32)
-                bias1 = small.tile([P, 1], F32)
-                norm_coefficients(
-                    nc,
-                    small,
-                    neg_half,
-                    moments1[:, 0:1],
-                    moments1[:, 1:2],
-                    params[:, BLOCKS + b : BLOCKS + b + 1],
-                    params[:, 2 * BLOCKS + b : 2 * BLOCKS + b + 1],
-                    scale1[:],
-                    bias1[:],
-                )
-                for lo in range(0, ROWS, NORM_COLS):
-                    nc.gpsimd.tensor_scalar(
-                        out=h[:, lo : lo + NORM_COLS],
-                        in0=h[:, lo : lo + NORM_COLS],
-                        scalar1=scale1[:, 0:1],
-                        scalar2=bias1[:, 0:1],
-                        op0=ALU.mult,
-                        op1=ALU.add,
-                    )
-                return h
-
-            def store_block(b, h):
-                for c in range(CHUNKS):
-                    o_ps = psum.tile([P, ROW_TILES, P], F32, tag="tr")
-                    for j in range(ROW_TILES):
-                        lo = c * CHUNK + j * P
-                        nc.tensor.transpose(
-                            out=o_ps[:, j, :], in_=h[:, lo : lo + P], identity=ident_f32[:]
-                        )
-                    o_sb = outs.tile([P, ROW_TILES, P], F32)
-                    if c % 2 == 0:
-                        nc.vector.tensor_copy(out=o_sb[:], in_=o_ps[:])
-                    else:
-                        nc.scalar.copy(out=o_sb[:], in_=o_ps[:])
-                    nc.sync.dma_start(out=out_view[c][:, :, b * P : (b + 1) * P], in_=o_sb[:])
-
-            previous = None
-            for b in range(BLOCKS):
-                h = linear_block(b)
-                if previous is not None:
-                    store_block(b - 1, previous)
-                previous = h
-            store_block(BLOCKS - 1, previous)
+        waiting = None
+        for b in range(BLOCKS):
+            h = linear_block(b)
+            if waiting is not None:
+                store_block(b - 1, waiting)
+            waiting = h
+        store_block(BLOCKS - 1, waiting)

@@ -23,19 +23,25 @@ ROW_TILES = CHUNK // P
 BLOCKS = D_OUT // P
 HALVES = 2
 BN_MAX = 512
+AFFINE_COLS = 2048
+NORM_COLS = 1024
+RUN = 4
+LAG = 3
 EPS = 1e-5
 
 FLOPS = 2 * ROWS * D_IN * D_OUT
 
 
-def norm_coefficients(nc, pool, mean, var, gain, shift, scale_out, bias_out, width):
-    std = pool.tile([P, width], F32)
-    nc.vector.tensor_scalar_add(out=std[:], in0=var, scalar1=EPS)
-    nc.scalar.activation(out=std[:], in_=std[:], func=ACT.Sqrt)
-    nc.vector.reciprocal(out=std[:], in_=std[:])
-    nc.vector.tensor_mul(out=scale_out, in0=gain, in1=std[:])
-    nc.vector.tensor_mul(out=std[:], in0=mean, in1=scale_out)
-    nc.vector.tensor_sub(out=bias_out, in0=shift, in1=std[:])
+def norm_coefficients(nc, pool, neg_half, mean, var, gain, shift, scale_out, bias_out):
+    width = scale_out.shape[1]
+    rstd = pool.tile([P, width], F32)
+    nc.gpsimd.tensor_scalar(
+        out=rstd[:], in0=var, scalar1=1.0, scalar2=EPS, op0=ALU.mult, op1=ALU.add
+    )
+    nc.gpsimd.tensor_tensor(out=rstd[:], in0=rstd[:], in1=neg_half[:, 0:width], op=ALU.pow)
+    nc.gpsimd.tensor_mul(out=scale_out, in0=gain, in1=rstd[:])
+    nc.gpsimd.tensor_mul(out=rstd[:], in0=mean, in1=scale_out)
+    nc.gpsimd.tensor_sub(out=bias_out, in0=shift, in1=rstd[:])
 
 
 def tile_settransform_pa_t_kernel(
@@ -50,208 +56,223 @@ def tile_settransform_pa_t_kernel(
     )
 
     with tc.tile_pool(name="keep", bufs=1) as keep, tc.tile_pool(
-        name="xin", bufs=4
-    ) as xin, tc.tile_pool(name="stage", bufs=3) as stage, tc.tile_pool(
-        name="hidden", bufs=3
-    ) as hidden, tc.tile_pool(name="small", bufs=4) as small, tc.tile_pool(
-        name="outs", bufs=4
-    ) as outs, tc.psum_pool(name="psum", bufs=4) as psum:
-        warm = keep.tile([P, 1], F32)
-        nc.vector.memset(warm[:], 1.0)
-        nc.scalar.activation(out=warm[:], in_=warm[:], func=ACT.Sqrt)
-
+        name="small", bufs=4
+    ) as small, tc.psum_pool(name="psum", bufs=4) as psum, tc.manual_schedule():
         ident_f32 = keep.tile([P, P], F32)
         make_identity(nc, ident_f32[:])
         ident_bf16 = keep.tile([P, P], BF16)
         make_identity(nc, ident_bf16[:])
+        neg_half = keep.tile([P, PACK], F32)
+        nc.gpsimd.memset(neg_half[:], -0.5)
 
         w_scales = keep.tile([P, PASSES, D_OUT], U8, align_bytes=64)
         nc.vector.memset(w_scales[:].rearrange("p g n -> p (g n)").bitcast(I32), 0)
         param_rows = keep.tile([P, P], BF16)
         nc.vector.memset(param_rows[:], 0.0)
 
-        gain0_bf = keep.tile([P, PASSES, PACK], BF16)
-        shift0_bf = keep.tile([P, PASSES, PACK], BF16)
-        nc.scalar.dma_start(
-            out=gain0_bf[:], in_=g0.rearrange("(g p t) -> p g t", g=PASSES, p=P)
-        )
-        nc.scalar.dma_start(
-            out=shift0_bf[:], in_=b0.rearrange("(g p t) -> p g t", g=PASSES, p=P)
-        )
+        gain0 = keep.tile([P, PASSES, PACK], BF16)
+        shift0 = keep.tile([P, PASSES, PACK], BF16)
+        nc.scalar.dma_start(out=gain0[:], in_=g0.rearrange("(g p t) -> p g t", g=PASSES, p=P))
+        nc.scalar.dma_start(out=shift0[:], in_=b0.rearrange("(g p t) -> p g t", g=PASSES, p=P))
         for v, vec in enumerate((c0, g1, b1)):
             nc.scalar.dma_start(
                 out=param_rows[v * BLOCKS : (v + 1) * BLOCKS, :],
                 in_=vec.rearrange("(b p) -> b p", p=P),
             )
-        gain0 = keep.tile([P, PASSES, PACK], F32)
-        shift0 = keep.tile([P, PASSES, PACK], F32)
-        nc.vector.tensor_copy(out=gain0[:], in_=gain0_bf[:])
-        nc.vector.tensor_copy(out=shift0[:], in_=shift0_bf[:])
-        params_ps = psum.tile([P, P], BF16, tag="tr")
-        nc.tensor.transpose(out=params_ps[:], in_=param_rows[:], identity=ident_bf16[:])
-        params = keep.tile([P, 3 * BLOCKS], F32)
-        nc.vector.tensor_copy(out=params[:], in_=params_ps[:, 0 : 3 * BLOCKS])
-
-        x_t = keep.tile([P, PASSES, HALVES, ROWS * 2], BF16)
-        pieces = ROWS * 2 // BN_MAX
-        stats0 = keep.tile([P, PASSES, HALVES, pieces, 6], F32)
-        moments0 = keep.tile([P, PASSES, PACK, 2], F32)
-        scale0 = keep.tile([P, PASSES, PACK], F32)
-        bias0 = keep.tile([P, PASSES, PACK], F32)
-        for g in range(PASSES):
-            for c in range(CHUNKS):
-                x_sb = xin.tile([P, ROW_TILES, K_PASS], BF16)
-                nc.sync.dma_start(
-                    out=x_sb[:], in_=x_view[c][:, :, g * K_PASS : (g + 1) * K_PASS]
-                )
-                for u in range(HALVES):
-                    x_ps = psum.tile([P, CHUNK], F32, tag="tr")
-                    for j in range(ROW_TILES):
-                        nc.tensor.transpose(
-                            out=x_ps[:, j * P : (j + 1) * P],
-                            in_=x_sb[:, j, :].bitcast(F32)[:, u : K_PASS // 2 : HALVES],
-                            identity=ident_f32[:],
-                        )
-                    lo = c * CHUNK * 2
-                    nc.scalar.copy(
-                        out=x_t[:, g, u, lo : lo + CHUNK * 2], in_=x_ps[:].bitcast(BF16)
-                    )
-                    for s in range(CHUNK * 2 // BN_MAX):
-                        piece = c * (CHUNK * 2 // BN_MAX) + s
-                        nc.vector.bn_stats(
-                            out=stats0[:, g, u, piece, :],
-                            in_=x_t[:, g, u, piece * BN_MAX : (piece + 1) * BN_MAX],
-                        )
-            for u in range(HALVES):
-                for e in range(2):
-                    nc.vector.bn_aggr(
-                        out=moments0[:, g, 2 * u + e, :],
-                        in_=stats0[:, g, u, :, 3 * e : 3 * e + 3],
-                    )
-            norm_coefficients(
-                nc,
-                small,
-                moments0[:, g, :, 0],
-                moments0[:, g, :, 1],
-                gain0[:, g, :],
-                shift0[:, g, :],
-                scale0[:, g, :],
-                bias0[:, g, :],
-                PACK,
-            )
 
         w_codes = keep.tile([P, PASSES, D_OUT], U32, align_bytes=64)
-        for g in range(PASSES):
-            nc.sync.dma_start(
-                out=w_codes[:, g, :].bitcast(I32),
-                in_=W0_words[g].rearrange("p n t -> p (n t)").bitcast(I32),
-            )
-        for g in range(PASSES):
-            for q in range(4):
-                nc.sync.dma_start(
-                    out=w_scales[32 * q : 32 * q + 4, g, :].bitcast(I32),
-                    in_=W0_scales[g, 4 * q : 4 * q + 4, :].bitcast(I32),
-                )
-
         x_codes = keep.tile([P, PASSES, ROWS], U32, align_bytes=64)
         x_scales = keep.tile([P, PASSES, ROWS], U8, align_bytes=64)
-        for g in range(PASSES):
-            for c in range(CHUNKS):
-                cols = slice(c * CHUNK, (c + 1) * CHUNK)
-                planes = stage.tile([P, PACK, CHUNK], BF16)
-                for u in range(HALVES):
-                    pairs = x_t[:, g, u, :].rearrange("p (c e) -> p c e", e=2)
-                    for e in range(2):
-                        t = 2 * u + e
-                        nc.scalar.activation(
-                            out=planes[:, t, :],
-                            in_=pairs[:, cols, e],
-                            func=ACT.Identity,
-                            scale=scale0[:, g, t : t + 1],
-                            bias=bias0[:, g, t : t + 1],
-                        )
-                grouped = stage.tile([P, CHUNK, PACK], BF16, align_bytes=64)
-                nc.vector.tensor_copy(
-                    out=grouped[:].rearrange("p (c i) t -> p c t i", i=4),
-                    in_=planes[:].rearrange("p t (c i) -> p c t i", i=4),
-                )
-                nc.vector.quantize_mx(
-                    out=x_codes[:, g, cols].bitcast(FP8X4),
-                    scales=x_scales[:, g, cols],
-                    in_=grouped[:].rearrange("p c t -> p (c t)"),
-                )
+        params = keep.tile([P, 3 * BLOCKS], F32)
 
-        def linear_block(b):
-            feats = slice(b * P, (b + 1) * P)
-            h = hidden.tile([P, ROWS], F32)
-            stats1 = small.tile([P, CHUNKS, 6], F32)
-            for c in range(CHUNKS):
-                cols = slice(c * CHUNK, (c + 1) * CHUNK)
-                acc = psum.tile([P, CHUNK], F32, tag="acc")
+        with tc.tile_pool(name="early", bufs=1) as early:
+            x_t = early.tile([P, PASSES, HALVES, ROWS * 2], BF16)
+            pieces = ROWS * 2 // BN_MAX
+            stats0 = early.tile([P, PASSES, HALVES, pieces, 6], F32)
+            moments0 = early.tile([P, PASSES, PACK, 2], F32)
+            scale0 = early.tile([P, PASSES, PACK], F32)
+            bias0 = early.tile([P, PASSES, PACK], F32)
+
+            with tc.tile_pool(name="xin", bufs=8) as xin:
                 for g in range(PASSES):
-                    nc.tensor.matmul_mx(
-                        out=acc[:],
-                        lhsT=w_codes[:, g, feats].bitcast(FP8X4),
-                        lhsT_scale=w_scales[:, g, feats],
-                        rhs=x_codes[:, g, cols].bitcast(FP8X4),
-                        rhs_scale=x_scales[:, g, cols],
-                        start=(g == 0),
-                        stop=(g == PASSES - 1),
+                    for c in range(CHUNKS):
+                        x_sb = xin.tile([P, ROW_TILES, K_PASS], BF16)
+                        nc.sync.dma_start(
+                            out=x_sb[:], in_=x_view[c][:, :, g * K_PASS : (g + 1) * K_PASS]
+                        )
+                        for u in range(HALVES):
+                            x_ps = psum.tile([P, CHUNK], F32, tag="tr")
+                            for j in range(ROW_TILES):
+                                nc.tensor.transpose(
+                                    out=x_ps[:, j * P : (j + 1) * P],
+                                    in_=x_sb[:, j, :].bitcast(F32)[:, u : K_PASS // 2 : HALVES],
+                                    identity=ident_f32[:],
+                                )
+                            lo = c * CHUNK * 2
+                            nc.scalar.copy(
+                                out=x_t[:, g, u, lo : lo + CHUNK * 2],
+                                in_=x_ps[:].bitcast(BF16),
+                            )
+                            for s in range(CHUNK * 2 // BN_MAX):
+                                piece = c * (CHUNK * 2 // BN_MAX) + s
+                                nc.vector.bn_stats(
+                                    out=stats0[:, g, u, piece, :],
+                                    in_=x_t[:, g, u, piece * BN_MAX : (piece + 1) * BN_MAX],
+                                )
+                    for u in range(HALVES):
+                        for e in range(2):
+                            nc.vector.bn_aggr(
+                                out=moments0[:, g, 2 * u + e, :],
+                                in_=stats0[:, g, u, :, 3 * e : 3 * e + 3],
+                            )
+                    norm_coefficients(
+                        nc,
+                        small,
+                        neg_half,
+                        moments0[:, g, :, 0],
+                        moments0[:, g, :, 1],
+                        gain0[:, g, :],
+                        shift0[:, g, :],
+                        scale0[:, g, :],
+                        bias0[:, g, :],
                     )
-                nc.scalar.activation(
-                    out=h[:, cols], in_=acc[:], func=ACT.Relu, bias=params[:, b : b + 1]
-                )
-                nc.vector.bn_stats(out=stats1[:, c, :], in_=h[:, cols])
-            moments1 = small.tile([P, 2], F32)
-            nc.vector.bn_aggr(
-                out=moments1[:], in_=stats1[:].rearrange("p c (s v) -> p (c s) v", v=3)
-            )
-            scale1 = small.tile([P, 1], F32)
-            bias1 = small.tile([P, 1], F32)
-            norm_coefficients(
-                nc,
-                small,
-                moments1[:, 0:1],
-                moments1[:, 1:2],
-                params[:, BLOCKS + b : BLOCKS + b + 1],
-                params[:, 2 * BLOCKS + b : 2 * BLOCKS + b + 1],
-                scale1[:],
-                bias1[:],
-                1,
-            )
-            for c in range(0, CHUNKS, 2):
-                cols = slice(c * CHUNK, (c + 2) * CHUNK)
-                nc.vector.tensor_scalar(
-                    out=h[:, cols],
-                    in0=h[:, cols],
-                    scalar1=scale1[:, 0:1],
-                    scalar2=bias1[:, 0:1],
-                    op0=ALU.mult,
-                    op1=ALU.add,
-                )
-            return h
 
-        def store_block(b, h):
-            for c in range(CHUNKS):
-                o_ps = psum.tile([P, ROW_TILES, P], F32, tag="tr")
-                for j in range(ROW_TILES):
-                    lo = c * CHUNK + j * P
-                    nc.tensor.transpose(
-                        out=o_ps[:, j, :], in_=h[:, lo : lo + P], identity=ident_f32[:]
-                    )
-                o_sb = outs.tile([P, ROW_TILES, P], F32)
-                if c % 2 == 0:
-                    nc.vector.tensor_copy(out=o_sb[:], in_=o_ps[:])
-                else:
-                    nc.scalar.copy(out=o_sb[:], in_=o_ps[:])
+            for g in range(PASSES):
                 nc.sync.dma_start(
-                    out=out_view[c][:, :, b * P : (b + 1) * P], in_=o_sb[:]
+                    out=w_codes[:, g, :].bitcast(I32),
+                    in_=W0_words[g].rearrange("p n t -> p (n t)").bitcast(I32),
                 )
+            for g in range(PASSES):
+                for q in range(4):
+                    nc.sync.dma_start(
+                        out=w_scales[32 * q : 32 * q + 4, g, :].bitcast(I32),
+                        in_=W0_scales[g, 4 * q : 4 * q + 4, :].bitcast(I32),
+                    )
+            params_ps = psum.tile([P, P], BF16, tag="tr")
+            nc.tensor.transpose(out=params_ps[:], in_=param_rows[:], identity=ident_bf16[:])
+            nc.vector.tensor_copy(out=params[:], in_=params_ps[:, 0 : 3 * BLOCKS])
 
-        waiting = None
-        for b in range(BLOCKS):
-            h = linear_block(b)
-            if waiting is not None:
-                store_block(b - 1, waiting)
-            waiting = h
-        store_block(BLOCKS - 1, waiting)
+            with tc.tile_pool(name="stage", bufs=2) as stage, tc.tile_pool(
+                name="words", bufs=3
+            ) as words:
+
+                def quantise(g, cols, grouped):
+                    nc.vector.quantize_mx(
+                        out=x_codes[:, g, cols].bitcast(FP8X4),
+                        scales=x_scales[:, g, cols],
+                        in_=grouped[:].rearrange("p c t -> p (c t)"),
+                    )
+
+                waiting = None
+                for g in range(PASSES):
+                    for a in range(ROWS // AFFINE_COLS):
+                        planes = stage.tile([P, PACK, AFFINE_COLS], BF16)
+                        for u in range(HALVES):
+                            pairs = x_t[:, g, u, :].rearrange("p (c e) -> p c e", e=2)
+                            for e in range(2):
+                                t = 2 * u + e
+                                nc.scalar.activation(
+                                    out=planes[:, t, :],
+                                    in_=pairs[:, a * AFFINE_COLS : (a + 1) * AFFINE_COLS, e],
+                                    func=ACT.Identity,
+                                    scale=scale0[:, g, t : t + 1],
+                                    bias=bias0[:, g, t : t + 1],
+                                )
+                        for s in range(AFFINE_COLS // CHUNK):
+                            grouped = words.tile([P, CHUNK, PACK], BF16, align_bytes=64)
+                            nc.vector.tensor_copy(
+                                out=grouped[:].rearrange("p (c i) t -> p c t i", i=4),
+                                in_=planes[:, :, s * CHUNK : (s + 1) * CHUNK].rearrange(
+                                    "p t (c i) -> p c t i", i=4
+                                ),
+                            )
+                            if waiting is not None:
+                                quantise(*waiting)
+                            lo = a * AFFINE_COLS + s * CHUNK
+                            waiting = (g, slice(lo, lo + CHUNK), grouped)
+                quantise(*waiting)
+
+        with tc.tile_pool(name="hidden", bufs=3) as hidden, tc.tile_pool(
+            name="outs", bufs=8
+        ) as outs:
+            h_tiles = {}
+            stats1_tiles = {}
+
+            def linear_half(b, half):
+                feats = slice(b * P, (b + 1) * P)
+                if half == 0:
+                    h_tiles[b] = hidden.tile([P, ROWS], F32, name="h")
+                    stats1_tiles[b] = small.tile([P, CHUNKS, 6], F32, name="stats1")
+                h = h_tiles[b]
+                stats1 = stats1_tiles[b]
+                for c in range(half * RUN, (half + 1) * RUN):
+                    cols = slice(c * CHUNK, (c + 1) * CHUNK)
+                    acc = psum.tile([P, CHUNK], F32, tag="acc")
+                    for g in range(PASSES):
+                        nc.tensor.matmul_mx(
+                            out=acc[:],
+                            lhsT=w_codes[:, g, feats].bitcast(FP8X4),
+                            lhsT_scale=w_scales[:, g, feats],
+                            rhs=x_codes[:, g, cols].bitcast(FP8X4),
+                            rhs_scale=x_scales[:, g, cols],
+                            start=(g == 0),
+                            stop=(g == PASSES - 1),
+                        )
+                    nc.scalar.activation(
+                        out=h[:, cols], in_=acc[:], func=ACT.Relu, bias=params[:, b : b + 1]
+                    )
+                    nc.vector.bn_stats(out=stats1[:, c, :], in_=h[:, cols])
+
+            def normalise(b):
+                h = h_tiles[b]
+                moments1 = small.tile([P, 2], F32)
+                nc.vector.bn_aggr(
+                    out=moments1[:],
+                    in_=stats1_tiles[b][:].rearrange("p c (s v) -> p (c s) v", v=3),
+                )
+                scale1 = small.tile([P, 1], F32)
+                bias1 = small.tile([P, 1], F32)
+                norm_coefficients(
+                    nc,
+                    small,
+                    neg_half,
+                    moments1[:, 0:1],
+                    moments1[:, 1:2],
+                    params[:, BLOCKS + b : BLOCKS + b + 1],
+                    params[:, 2 * BLOCKS + b : 2 * BLOCKS + b + 1],
+                    scale1[:],
+                    bias1[:],
+                )
+                for lo in range(0, ROWS, NORM_COLS):
+                    nc.gpsimd.tensor_scalar(
+                        out=h[:, lo : lo + NORM_COLS],
+                        in0=h[:, lo : lo + NORM_COLS],
+                        scalar1=scale1[:, 0:1],
+                        scalar2=bias1[:, 0:1],
+                        op0=ALU.mult,
+                        op1=ALU.add,
+                    )
+
+            def store_half(b, half):
+                h = h_tiles[b]
+                for c in range(half * RUN, (half + 1) * RUN):
+                    o_ps = psum.tile([P, ROW_TILES, P], F32, tag="tr")
+                    for j in range(ROW_TILES):
+                        lo = c * CHUNK + j * P
+                        nc.tensor.transpose(
+                            out=o_ps[:, j, :], in_=h[:, lo : lo + P], identity=ident_f32[:]
+                        )
+                    o_sb = outs.tile([P, ROW_TILES, P], F32)
+                    if c % 2 == 0:
+                        nc.vector.tensor_copy(out=o_sb[:], in_=o_ps[:])
+                    else:
+                        nc.scalar.copy(out=o_sb[:], in_=o_ps[:])
+                    nc.sync.dma_start(out=out_view[c][:, :, b * P : (b + 1) * P], in_=o_sb[:])
+
+            for k in range(2 * BLOCKS + LAG):
+                if k < 2 * BLOCKS:
+                    linear_half(k // 2, k % 2)
+                    if k % 2 == 1:
+                        normalise(k // 2)
+                if k >= LAG:
+                    store_half((k - LAG) // 2, (k - LAG) % 2)

@@ -23,7 +23,9 @@ ROW_TILES = CHUNK // P
 BLOCKS = D_OUT // P
 HALVES = 2
 BN_MAX = 512
-AFFINE_COLS = 2048
+AFFINE_COLS = 1024
+PIECES = ROWS // AFFINE_COLS
+GPSIMD_PIECES = 3
 NORM_COLS = 1024
 RUN = 4
 LAG = 3
@@ -93,8 +95,12 @@ def tile_settransform_pa_t_kernel(
             scale0 = early.tile([P, PASSES, PACK], F32)
             bias0 = early.tile([P, PASSES, PACK], F32)
 
-            with tc.tile_pool(name="xin", bufs=8) as xin:
-                for g in range(PASSES):
+            with tc.tile_pool(name="xin", bufs=8) as xin, tc.tile_pool(
+                name="stage", bufs=PASSES * PIECES
+            ) as stage, tc.tile_pool(name="words", bufs=3) as words:
+                planes_tiles = {}
+
+                def statistics(g):
                     for c in range(CHUNKS):
                         x_sb = xin.tile([P, ROW_TILES, K_PASS], BF16)
                         nc.sync.dma_start(
@@ -137,24 +143,31 @@ def tile_settransform_pa_t_kernel(
                         bias0[:, g, :],
                     )
 
-            for g in range(PASSES):
-                nc.sync.dma_start(
-                    out=w_codes[:, g, :].bitcast(I32),
-                    in_=W0_words[g].rearrange("p n t -> p (n t)").bitcast(I32),
-                )
-            for g in range(PASSES):
-                for q in range(4):
-                    nc.sync.dma_start(
-                        out=w_scales[32 * q : 32 * q + 4, g, :].bitcast(I32),
-                        in_=W0_scales[g, 4 * q : 4 * q + 4, :].bitcast(I32),
-                    )
-            params_ps = psum.tile([P, P], BF16, tag="tr")
-            nc.tensor.transpose(out=params_ps[:], in_=param_rows[:], identity=ident_bf16[:])
-            nc.vector.tensor_copy(out=params[:], in_=params_ps[:, 0 : 3 * BLOCKS])
-
-            with tc.tile_pool(name="stage", bufs=2) as stage, tc.tile_pool(
-                name="words", bufs=3
-            ) as words:
+                def affine(g, a, on_gpsimd):
+                    planes = stage.tile([P, PACK, AFFINE_COLS], BF16, name="planes")
+                    planes_tiles[(g, a)] = planes
+                    for u in range(HALVES):
+                        pairs = x_t[:, g, u, :].rearrange("p (c e) -> p c e", e=2)
+                        for e in range(2):
+                            t = 2 * u + e
+                            rows = pairs[:, a * AFFINE_COLS : (a + 1) * AFFINE_COLS, e]
+                            if on_gpsimd:
+                                nc.gpsimd.tensor_scalar(
+                                    out=planes[:, t, :],
+                                    in0=rows,
+                                    scalar1=scale0[:, g, t : t + 1],
+                                    scalar2=bias0[:, g, t : t + 1],
+                                    op0=ALU.mult,
+                                    op1=ALU.add,
+                                )
+                            else:
+                                nc.scalar.activation(
+                                    out=planes[:, t, :],
+                                    in_=rows,
+                                    func=ACT.Identity,
+                                    scale=scale0[:, g, t : t + 1],
+                                    bias=bias0[:, g, t : t + 1],
+                                )
 
                 def quantise(g, cols, grouped):
                     nc.vector.quantize_mx(
@@ -163,21 +176,35 @@ def tile_settransform_pa_t_kernel(
                         in_=grouped[:].rearrange("p c t -> p (c t)"),
                     )
 
+                statistics(0)
+                for a in range(GPSIMD_PIECES):
+                    affine(0, a, True)
+                statistics(1)
+                for a in range(GPSIMD_PIECES, PIECES):
+                    affine(0, a, False)
+
+                for g in range(PASSES):
+                    nc.sync.dma_start(
+                        out=w_codes[:, g, :].bitcast(I32),
+                        in_=W0_words[g].rearrange("p n t -> p (n t)").bitcast(I32),
+                    )
+                for g in range(PASSES):
+                    for q in range(4):
+                        nc.sync.dma_start(
+                            out=w_scales[32 * q : 32 * q + 4, g, :].bitcast(I32),
+                            in_=W0_scales[g, 4 * q : 4 * q + 4, :].bitcast(I32),
+                        )
+                params_ps = psum.tile([P, P], BF16, tag="tr")
+                nc.tensor.transpose(out=params_ps[:], in_=param_rows[:], identity=ident_bf16[:])
+                nc.vector.tensor_copy(out=params[:], in_=params_ps[:, 0 : 3 * BLOCKS])
+
+                for a in range(PIECES):
+                    affine(1, a, False)
+
                 waiting = None
                 for g in range(PASSES):
-                    for a in range(ROWS // AFFINE_COLS):
-                        planes = stage.tile([P, PACK, AFFINE_COLS], BF16)
-                        for u in range(HALVES):
-                            pairs = x_t[:, g, u, :].rearrange("p (c e) -> p c e", e=2)
-                            for e in range(2):
-                                t = 2 * u + e
-                                nc.scalar.activation(
-                                    out=planes[:, t, :],
-                                    in_=pairs[:, a * AFFINE_COLS : (a + 1) * AFFINE_COLS, e],
-                                    func=ACT.Identity,
-                                    scale=scale0[:, g, t : t + 1],
-                                    bias=bias0[:, g, t : t + 1],
-                                )
+                    for a in range(PIECES):
+                        planes = planes_tiles[(g, a)]
                         for s in range(AFFINE_COLS // CHUNK):
                             grouped = words.tile([P, CHUNK, PACK], BF16, align_bytes=64)
                             nc.vector.tensor_copy(

@@ -99,6 +99,9 @@ def tile_settransform_pa_t_kernel(
                 name="stage", bufs=PASSES * PIECES
             ) as stage, tc.tile_pool(name="words", bufs=3) as words:
                 planes_tiles = {}
+                idle_in = early.tile([P, CHUNK], BF16)
+                nc.vector.memset(idle_in[:], 0.0)
+                idle_out = psum.tile([P, CHUNK], F32, tag="acc")
 
                 def statistics(g):
                     for c in range(CHUNKS):
@@ -114,10 +117,13 @@ def tile_settransform_pa_t_kernel(
                                     in_=x_sb[:, j, :].bitcast(F32)[:, u : K_PASS // 2 : HALVES],
                                     identity=ident_f32[:],
                                 )
+                            nc.tensor.matmul(
+                                out=idle_out[:], lhsT=ident_bf16[:], rhs=idle_in[:], start=True, stop=True
+                            )
                             lo = c * CHUNK * 2
                             nc.scalar.copy(
-                                out=x_t[:, g, u, lo : lo + CHUNK * 2],
-                                in_=x_ps[:].bitcast(BF16),
+                                out=x_t[:, g, u, lo : lo + CHUNK * 2].bitcast(F32),
+                                in_=x_ps[:],
                             )
                             for s in range(CHUNK * 2 // BN_MAX):
                                 piece = c * (CHUNK * 2 // BN_MAX) + s

@@ -26,6 +26,7 @@ BN_MAX = 512
 AFFINE_COLS = 1024
 PIECES = ROWS // AFFINE_COLS
 GPSIMD_PIECES = 3
+SCALAR_CHUNKS = (6, 7, 0, 1, 2)
 NORM_COLS = 1024
 RUN = 4
 LAG = 3
@@ -95,13 +96,16 @@ def tile_settransform_pa_t_kernel(
             scale0 = early.tile([P, PASSES, PACK], F32)
             bias0 = early.tile([P, PASSES, PACK], F32)
 
-            with tc.tile_pool(name="xin", bufs=8) as xin, tc.tile_pool(
-                name="stage", bufs=PASSES * PIECES
-            ) as stage, tc.tile_pool(name="words", bufs=3) as words:
+            with tc.tile_pool(name="xin", bufs=6) as xin, tc.tile_pool(
+                name="stage", bufs=6
+            ) as stage, tc.tile_pool(name="words", bufs=3) as words, tc.tile_pool(
+                name="early_words", bufs=len(SCALAR_CHUNKS)
+            ) as early_words:
                 planes_tiles = {}
                 idle_in = early.tile([P, CHUNK], BF16)
                 nc.vector.memset(idle_in[:], 0.0)
                 idle_out = psum.tile([P, CHUNK], F32, tag="acc")
+                early_tiles = {}
 
                 def statistics(g):
                     for c in range(CHUNKS):
@@ -188,6 +192,16 @@ def tile_settransform_pa_t_kernel(
                 statistics(1)
                 for a in range(GPSIMD_PIECES, PIECES):
                     affine(0, a, False)
+                for c in SCALAR_CHUNKS:
+                    a, s = divmod(c, AFFINE_COLS // CHUNK)
+                    laid = early_words.tile([P, CHUNK, PACK], BF16, align_bytes=64)
+                    early_tiles[c] = laid
+                    nc.scalar.copy(
+                        out=laid[:],
+                        in_=planes_tiles[(0, a)][:, :, s * CHUNK : (s + 1) * CHUNK].rearrange(
+                            "p t c -> p c t"
+                        ),
+                    )
 
                 for g in range(PASSES):
                     nc.sync.dma_start(
@@ -207,11 +221,15 @@ def tile_settransform_pa_t_kernel(
                 for a in range(PIECES):
                     affine(1, a, False)
 
+                for c in SCALAR_CHUNKS:
+                    quantise(0, slice(c * CHUNK, (c + 1) * CHUNK), early_tiles[c])
                 waiting = None
                 for g in range(PASSES):
                     for a in range(PIECES):
                         planes = planes_tiles[(g, a)]
                         for s in range(AFFINE_COLS // CHUNK):
+                            if g == 0 and a * (AFFINE_COLS // CHUNK) + s in SCALAR_CHUNKS:
+                                continue
                             grouped = words.tile([P, CHUNK, PACK], BF16, align_bytes=64)
                             nc.vector.tensor_copy(
                                 out=grouped[:].rearrange("p (c i) t -> p c t i", i=4),

@@ -23,10 +23,14 @@ ROW_TILES = CHUNK // P
 BLOCKS = D_OUT // P
 HALVES = 2
 BN_MAX = 512
-AFFINE_COLS = 1024
-PIECES = ROWS // AFFINE_COLS
-GPSIMD_PIECES = 3
-SCALAR_CHUNKS = (6, 7, 0, 1, 2)
+PIECE = 1024
+PIECES = ROWS // PIECE
+BN_CHUNKS = 2
+GRAM_CHUNKS = CHUNKS - BN_CHUNKS
+PAD = 8
+GRAM_COLS = P + 1
+BANKS = 4
+VECTOR_PLANE = 3
 NORM_COLS = 1024
 RUN = 4
 LAG = 3
@@ -39,7 +43,7 @@ def norm_coefficients(nc, pool, neg_half, mean, var, gain, shift, scale_out, bia
     width = scale_out.shape[1]
     rstd = pool.tile([P, width], F32)
     nc.gpsimd.tensor_scalar(
-        out=rstd[:], in0=var, scalar1=1.0, scalar2=EPS, op0=ALU.mult, op1=ALU.add
+        out=rstd[:], in0=var, scalar1=0.0, scalar2=EPS, op0=ALU.max, op1=ALU.add
     )
     nc.gpsimd.tensor_tensor(out=rstd[:], in0=rstd[:], in1=neg_half[:, 0:width], op=ALU.pow)
     nc.gpsimd.tensor_mul(out=scale_out, in0=gain, in1=rstd[:])
@@ -60,7 +64,11 @@ def tile_settransform_pa_t_kernel(
 
     with tc.tile_pool(name="keep", bufs=1) as keep, tc.tile_pool(
         name="small", bufs=4
-    ) as small, tc.psum_pool(name="psum", bufs=4) as psum, tc.manual_schedule():
+    ) as small, tc.psum_pool(name="psum", bufs=1) as psum, tc.manual_schedule():
+
+        def bank(i, shape, dtype):
+            return psum.tile(shape, dtype, name="bank%d" % i)
+
         ident_f32 = keep.tile([P, P], F32)
         make_identity(nc, ident_f32[:])
         ident_bf16 = keep.tile([P, P], BF16)
@@ -88,160 +96,225 @@ def tile_settransform_pa_t_kernel(
         x_scales = keep.tile([P, PASSES, ROWS], U8, align_bytes=64)
         params = keep.tile([P, 3 * BLOCKS], F32)
 
-        with tc.tile_pool(name="early", bufs=1) as early:
-            x_t = early.tile([P, PASSES, HALVES, ROWS * 2], BF16)
-            pieces = ROWS * 2 // BN_MAX
-            stats0 = early.tile([P, PASSES, HALVES, pieces, 6], F32)
+        with tc.tile_pool(name="early", bufs=1) as early, tc.tile_pool(
+            name="xin", bufs=PASSES * CHUNKS
+        ) as xin, tc.tile_pool(name="stage", bufs=5) as stage, tc.tile_pool(
+            name="words", bufs=3
+        ) as words:
+            stats0 = early.tile([P, PASSES, PACK, BN_CHUNKS, 6], F32)
             moments0 = early.tile([P, PASSES, PACK, 2], F32)
+            squares0 = early.tile([P, PASSES, PACK], F32)
+            mean0 = early.tile([P, PASSES, PACK], F32)
+            part0 = early.tile([P, PASSES, 2, PACK], F32)
+            var0 = early.tile([P, PASSES, PACK], F32)
             scale0 = early.tile([P, PASSES, PACK], F32)
             bias0 = early.tile([P, PASSES, PACK], F32)
+            product = early.tile([P, P], F32)
 
-            with tc.tile_pool(name="xin", bufs=6) as xin, tc.tile_pool(
-                name="stage", bufs=6
-            ) as stage, tc.tile_pool(name="words", bufs=3) as words, tc.tile_pool(
-                name="early_words", bufs=len(SCALAR_CHUNKS)
-            ) as early_words:
-                planes_tiles = {}
-                idle_in = early.tile([P, CHUNK], BF16)
-                nc.vector.memset(idle_in[:], 0.0)
-                idle_out = psum.tile([P, CHUNK], F32, tag="acc")
-                early_tiles = {}
-
-                def statistics(g):
-                    for c in range(CHUNKS):
-                        x_sb = xin.tile([P, ROW_TILES, K_PASS], BF16)
-                        nc.sync.dma_start(
-                            out=x_sb[:], in_=x_view[c][:, :, g * K_PASS : (g + 1) * K_PASS]
-                        )
-                        for u in range(HALVES):
-                            x_ps = psum.tile([P, CHUNK], F32, tag="tr")
-                            for j in range(ROW_TILES):
-                                nc.tensor.transpose(
-                                    out=x_ps[:, j * P : (j + 1) * P],
-                                    in_=x_sb[:, j, :].bitcast(F32)[:, u : K_PASS // 2 : HALVES],
-                                    identity=ident_f32[:],
-                                )
-                            nc.tensor.matmul(
-                                out=idle_out[:], lhsT=ident_bf16[:], rhs=idle_in[:], start=True, stop=True
-                            )
-                            lo = c * CHUNK * 2
-                            nc.scalar.copy(
-                                out=x_t[:, g, u, lo : lo + CHUNK * 2].bitcast(F32),
-                                in_=x_ps[:],
-                            )
-                            for s in range(CHUNK * 2 // BN_MAX):
-                                piece = c * (CHUNK * 2 // BN_MAX) + s
-                                nc.vector.bn_stats(
-                                    out=stats0[:, g, u, piece, :],
-                                    in_=x_t[:, g, u, piece * BN_MAX : (piece + 1) * BN_MAX],
-                                )
-                    for u in range(HALVES):
-                        for e in range(2):
-                            nc.vector.bn_aggr(
-                                out=moments0[:, g, 2 * u + e, :],
-                                in_=stats0[:, g, u, :, 3 * e : 3 * e + 3],
-                            )
-                    norm_coefficients(
-                        nc,
-                        small,
-                        neg_half,
-                        moments0[:, g, :, 0],
-                        moments0[:, g, :, 1],
-                        gain0[:, g, :],
-                        shift0[:, g, :],
-                        scale0[:, g, :],
-                        bias0[:, g, :],
-                    )
-
-                def affine(g, a, on_gpsimd):
-                    planes = stage.tile([P, PACK, AFFINE_COLS], BF16, name="planes")
-                    planes_tiles[(g, a)] = planes
-                    for u in range(HALVES):
-                        pairs = x_t[:, g, u, :].rearrange("p (c e) -> p c e", e=2)
-                        for e in range(2):
-                            t = 2 * u + e
-                            rows = pairs[:, a * AFFINE_COLS : (a + 1) * AFFINE_COLS, e]
-                            if on_gpsimd:
-                                nc.gpsimd.tensor_scalar(
-                                    out=planes[:, t, :],
-                                    in0=rows,
-                                    scalar1=scale0[:, g, t : t + 1],
-                                    scalar2=bias0[:, g, t : t + 1],
-                                    op0=ALU.mult,
-                                    op1=ALU.add,
-                                )
-                            else:
-                                nc.scalar.activation(
-                                    out=planes[:, t, :],
-                                    in_=rows,
-                                    func=ACT.Identity,
-                                    scale=scale0[:, g, t : t + 1],
-                                    bias=bias0[:, g, t : t + 1],
-                                )
-
-                def quantise(g, cols, grouped):
-                    nc.vector.quantize_mx(
-                        out=x_codes[:, g, cols].bitcast(FP8X4),
-                        scales=x_scales[:, g, cols],
-                        in_=grouped[:].rearrange("p c t -> p (c t)"),
-                    )
-
-                statistics(0)
-                for a in range(GPSIMD_PIECES):
-                    affine(0, a, True)
-                statistics(1)
-                for a in range(GPSIMD_PIECES, PIECES):
-                    affine(0, a, False)
-                for c in SCALAR_CHUNKS:
-                    a, s = divmod(c, AFFINE_COLS // CHUNK)
-                    laid = early_words.tile([P, CHUNK, PACK], BF16, align_bytes=64)
-                    early_tiles[c] = laid
-                    nc.scalar.copy(
-                        out=laid[:],
-                        in_=planes_tiles[(0, a)][:, :, s * CHUNK : (s + 1) * CHUNK].rearrange(
-                            "p t c -> p c t"
-                        ),
-                    )
-
-                for g in range(PASSES):
+            x_tiles = {}
+            for g in range(PASSES):
+                for c in range(CHUNKS):
+                    x_sb = xin.tile([P, ROW_TILES, K_PASS + PAD], BF16, name="x_sb")
+                    x_tiles[(g, c)] = x_sb
+                    if c >= BN_CHUNKS:
+                        nc.gpsimd.memset(x_sb[:, :, K_PASS:], 1.0)
                     nc.sync.dma_start(
-                        out=w_codes[:, g, :].bitcast(I32),
-                        in_=W0_words[g].rearrange("p n t -> p (n t)").bitcast(I32),
+                        out=x_sb[:, :, 0:K_PASS],
+                        in_=x_view[c][:, :, g * K_PASS : (g + 1) * K_PASS],
                     )
-                for g in range(PASSES):
-                    for q in range(4):
-                        nc.sync.dma_start(
-                            out=w_scales[32 * q : 32 * q + 4, g, :].bitcast(I32),
-                            in_=W0_scales[g, 4 * q : 4 * q + 4, :].bitcast(I32),
-                        )
-                params_ps = psum.tile([P, P], BF16, tag="tr")
-                nc.tensor.transpose(out=params_ps[:], in_=param_rows[:], identity=ident_bf16[:])
-                nc.vector.tensor_copy(out=params[:], in_=params_ps[:, 0 : 3 * BLOCKS])
+            for g in range(PASSES):
+                nc.sync.dma_start(
+                    out=w_codes[:, g, :].bitcast(I32),
+                    in_=W0_words[g].rearrange("p n t -> p (n t)").bitcast(I32),
+                )
+            for g in range(PASSES):
+                for q in range(4):
+                    nc.sync.dma_start(
+                        out=w_scales[32 * q : 32 * q + 4, g, :].bitcast(I32),
+                        in_=W0_scales[g, 4 * q : 4 * q + 4, :].bitcast(I32),
+                    )
 
-                for a in range(PIECES):
-                    affine(1, a, False)
+            def turn(g, a, t, i):
+                x_ps = bank(i, [P, PIECE], BF16)
+                for k in range(PIECE // P):
+                    c, j = divmod(a * (PIECE // P) + k, ROW_TILES)
+                    nc.tensor.transpose(
+                        out=x_ps[:, k * P : (k + 1) * P],
+                        in_=x_tiles[(g, c)][:, j, t:K_PASS:PACK],
+                        identity=ident_bf16[:],
+                    )
+                return x_ps
 
-                for c in SCALAR_CHUNKS:
-                    quantise(0, slice(c * CHUNK, (c + 1) * CHUNK), early_tiles[c])
-                waiting = None
-                for g in range(PASSES):
-                    for a in range(PIECES):
-                        planes = planes_tiles[(g, a)]
-                        for s in range(AFFINE_COLS // CHUNK):
-                            if g == 0 and a * (AFFINE_COLS // CHUNK) + s in SCALAR_CHUNKS:
-                                continue
-                            grouped = words.tile([P, CHUNK, PACK], BF16, align_bytes=64)
-                            nc.vector.tensor_copy(
-                                out=grouped[:].rearrange("p (c i) t -> p c t i", i=4),
-                                in_=planes[:, :, s * CHUNK : (s + 1) * CHUNK].rearrange(
-                                    "p t (c i) -> p c t i", i=4
-                                ),
-                            )
-                            if waiting is not None:
-                                quantise(*waiting)
-                            lo = a * AFFINE_COLS + s * CHUNK
-                            waiting = (g, slice(lo, lo + CHUNK), grouped)
-                quantise(*waiting)
+            def bank_statistics(g, t, x_ps):
+                for s in range(BN_CHUNKS):
+                    nc.vector.bn_stats(
+                        out=stats0[:, g, t, s, :], in_=x_ps[:, s:PIECE:BN_CHUNKS]
+                    )
+
+            def first_part(g):
+                for t in range(PACK):
+                    nc.vector.bn_aggr(
+                        out=moments0[:, g, t, :],
+                        in_=stats0[:, g, t, :, :].rearrange("p s (h v) -> p (s h) v", v=3),
+                    )
+                share = BN_CHUNKS / CHUNKS
+                mean, var = moments0[:, g, :, 0], moments0[:, g, :, 1]
+                nc.gpsimd.tensor_mul(out=part0[:, g, 1, :], in0=mean, in1=mean)
+                nc.gpsimd.tensor_add(out=part0[:, g, 1, :], in0=part0[:, g, 1, :], in1=var)
+                nc.gpsimd.tensor_scalar(
+                    out=part0[:, g, 1, :],
+                    in0=part0[:, g, 1, :],
+                    scalar1=share,
+                    scalar2=0.0,
+                    op0=ALU.mult,
+                    op1=ALU.add,
+                )
+                nc.gpsimd.tensor_scalar(
+                    out=part0[:, g, 0, :],
+                    in0=mean,
+                    scalar1=share,
+                    scalar2=0.0,
+                    op0=ALU.mult,
+                    op1=ALU.add,
+                )
+
+            def sums(g, c, j, grams):
+                x_sb = x_tiles[(g, c)]
+                for t in range(PACK):
+                    nc.tensor.matmul(
+                        out=grams[t][:, 0:GRAM_COLS],
+                        lhsT=x_sb[:, j, t:K_PASS:PACK],
+                        rhs=x_sb[:, j, t : K_PASS + t + 1 : PACK],
+                        start=(c == BN_CHUNKS and j == 0),
+                        stop=(c == CHUNKS - 1 and j == ROW_TILES - 1),
+                    )
+
+            def coefficients(g, grams):
+                for t in range(PACK):
+                    nc.vector.scalar_tensor_tensor(
+                        out=product[:],
+                        in0=grams[t][:, 0:P],
+                        scalar=1.0 / ROWS,
+                        in1=ident_f32[:],
+                        op0=ALU.mult,
+                        op1=ALU.mult,
+                        accum_out=squares0[:, g, t : t + 1],
+                    )
+                    nc.vector.scalar_tensor_tensor(
+                        out=mean0[:, g, t : t + 1],
+                        in0=grams[t][:, P:GRAM_COLS],
+                        scalar=1.0 / ROWS,
+                        in1=part0[:, g, 0, t : t + 1],
+                        op0=ALU.mult,
+                        op1=ALU.add,
+                    )
+                nc.vector.tensor_add(out=var0[:, g, :], in0=squares0[:, g, :], in1=part0[:, g, 1, :])
+                nc.vector.tensor_mul(out=part0[:, g, 0, :], in0=mean0[:, g, :], in1=mean0[:, g, :])
+                nc.vector.tensor_sub(out=var0[:, g, :], in0=var0[:, g, :], in1=part0[:, g, 0, :])
+                norm_coefficients(
+                    nc,
+                    small,
+                    neg_half,
+                    mean0[:, g, :],
+                    var0[:, g, :],
+                    gain0[:, g, :],
+                    shift0[:, g, :],
+                    scale0[:, g, :],
+                    bias0[:, g, :],
+                )
+
+            planes_tiles = {}
+
+            def affine(g, a, t, x_ps, on_vector=False):
+                if (g, a) not in planes_tiles:
+                    planes_tiles[(g, a)] = stage.tile([P, PACK, PIECE], BF16, name="planes")
+                out_plane = planes_tiles[(g, a)][:, t, :]
+                if on_vector:
+                    nc.vector.tensor_scalar(
+                        out=out_plane,
+                        in0=x_ps[:],
+                        scalar1=scale0[:, g, t : t + 1],
+                        scalar2=bias0[:, g, t : t + 1],
+                        op0=ALU.mult,
+                        op1=ALU.add,
+                    )
+                else:
+                    nc.scalar.activation(
+                        out=out_plane,
+                        in_=x_ps[:],
+                        func=ACT.Identity,
+                        scale=scale0[:, g, t : t + 1],
+                        bias=bias0[:, g, t : t + 1],
+                    )
+
+            waiting = []
+
+            def quantise():
+                g, cols, grouped = waiting[0]
+                waiting.clear()
+                nc.vector.quantize_mx(
+                    out=x_codes[:, g, cols].bitcast(FP8X4),
+                    scales=x_scales[:, g, cols],
+                    in_=grouped[:].rearrange("p c t -> p (c t)"),
+                )
+
+            def group(g, c):
+                a, s = divmod(c, PIECE // CHUNK)
+                grouped = words.tile([P, CHUNK, PACK], BF16, align_bytes=64)
+                nc.vector.tensor_copy(
+                    out=grouped[:].rearrange("p (c i) t -> p c t i", i=4),
+                    in_=planes_tiles[(g, a)][:, :, s * CHUNK : (s + 1) * CHUNK].rearrange(
+                        "p t (c i) -> p c t i", i=4
+                    ),
+                )
+                if waiting:
+                    quantise()
+                waiting.append((g, slice(c * CHUNK, (c + 1) * CHUNK), grouped))
+
+            held = {}
+            for t in range(PACK):
+                held[t] = turn(0, 0, t, t)
+                bank_statistics(0, t, held[t])
+            first_part(0)
+            grams0 = [bank(BANKS + t, [P, CHUNK], F32) for t in range(PACK)]
+            for c in range(BN_CHUNKS, CHUNKS):
+                for j in range(ROW_TILES):
+                    sums(0, c, j, grams0)
+            coefficients(0, grams0)
+
+            for t in range(PACK):
+                bank_statistics(1, t, turn(1, 0, t, BANKS + t))
+            first_part(1)
+
+            for t in range(PACK):
+                affine(0, 0, t, held[t])
+            for t in range(PACK):
+                affine(0, 1, t, turn(0, 1, t, t))
+            grams1 = [bank(BANKS + t, [P, CHUNK], F32) for t in range(PACK)]
+            row_tiles = [(c, j) for c in range(BN_CHUNKS, CHUNKS) for j in range(ROW_TILES)]
+            share = len(row_tiles) // (2 * PACK)
+            for n in range(2 * PACK):
+                for c, j in row_tiles[n * share : (n + 1) * share]:
+                    sums(1, c, j, grams1)
+                a, t = 2 + n // PACK, n % PACK
+                affine(0, a, t, turn(0, a, t, t))
+            for c in range(6):
+                group(0, c)
+            coefficients(1, grams1)
+            for c in range(6, CHUNKS):
+                group(0, c)
+
+            for a in range(PIECES):
+                for t in range(PACK):
+                    x_ps = turn(1, a, t, (a % 2) * BANKS + t)
+                    affine(1, a, t, x_ps, t == VECTOR_PLANE)
+                for c in (2 * a, 2 * a + 1):
+                    group(1, c)
+            quantise()
+
+            params_ps = bank(BANKS, [P, PIECE], BF16)
+            nc.tensor.transpose(out=params_ps[:, 0:P], in_=param_rows[:], identity=ident_bf16[:])
+            nc.vector.tensor_copy(out=params[:], in_=params_ps[:, 0 : 3 * BLOCKS])
 
         with tc.tile_pool(name="hidden", bufs=3) as hidden, tc.tile_pool(
             name="outs", bufs=8
@@ -258,7 +331,7 @@ def tile_settransform_pa_t_kernel(
                 stats1 = stats1_tiles[b]
                 for c in range(half * RUN, (half + 1) * RUN):
                     cols = slice(c * CHUNK, (c + 1) * CHUNK)
-                    acc = psum.tile([P, CHUNK], F32, tag="acc")
+                    acc = bank(BANKS + c % BANKS, [P, CHUNK], F32)
                     for g in range(PASSES):
                         nc.tensor.matmul_mx(
                             out=acc[:],
@@ -307,7 +380,7 @@ def tile_settransform_pa_t_kernel(
             def store_half(b, half):
                 h = h_tiles[b]
                 for c in range(half * RUN, (half + 1) * RUN):
-                    o_ps = psum.tile([P, ROW_TILES, P], F32, tag="tr")
+                    o_ps = bank(c % BANKS, [P, ROW_TILES, P], F32)
                     for j in range(ROW_TILES):
                         lo = c * CHUNK + j * P
                         nc.tensor.transpose(

@@ -9,6 +9,7 @@ U8 = mybir.dt.uint8
 FP8X4 = mybir.dt.float8_e4m3fn_x4
 ACT = mybir.ActivationFunctionType
 ALU = mybir.AluOpType
+AXIS = mybir.AxisListType
 
 P = 128
 PACK = 4
@@ -23,14 +24,13 @@ ROW_TILES = CHUNK // P
 BLOCKS = D_OUT // P
 HALVES = 2
 BN_MAX = 512
-PIECE = 1024
-PIECES = ROWS // PIECE
-BN_CHUNKS = 2
-GRAM_CHUNKS = CHUNKS - BN_CHUNKS
-PAD = 8
-GRAM_COLS = P + 1
+BN_CHUNKS = (0, 1, 2, 4)
+SUM_CHUNKS = ((3, 5, 6, 7), tuple(range(CHUNKS)))
+K_BLOCKS = K_PASS // P
+WORD_BANKS = 3
+SUM_BANK = 3
 BANKS = 4
-VECTOR_PLANE = 3
+AHEAD = 20
 NORM_COLS = 1024
 RUN = 4
 LAG = 3
@@ -39,16 +39,16 @@ EPS = 1e-5
 FLOPS = 2 * ROWS * D_IN * D_OUT
 
 
-def norm_coefficients(nc, pool, neg_half, mean, var, gain, shift, scale_out, bias_out):
+def norm_coefficients(nc, engine, pool, neg_half, mean, var, gain, shift, scale_out, bias_out):
     width = scale_out.shape[1]
     rstd = pool.tile([P, width], F32)
-    nc.gpsimd.tensor_scalar(
+    engine.tensor_scalar(
         out=rstd[:], in0=var, scalar1=0.0, scalar2=EPS, op0=ALU.max, op1=ALU.add
     )
     nc.gpsimd.tensor_tensor(out=rstd[:], in0=rstd[:], in1=neg_half[:, 0:width], op=ALU.pow)
-    nc.gpsimd.tensor_mul(out=scale_out, in0=gain, in1=rstd[:])
-    nc.gpsimd.tensor_mul(out=rstd[:], in0=mean, in1=scale_out)
-    nc.gpsimd.tensor_sub(out=bias_out, in0=shift, in1=rstd[:])
+    engine.tensor_mul(out=scale_out, in0=gain, in1=rstd[:])
+    engine.tensor_mul(out=rstd[:], in0=mean, in1=scale_out)
+    engine.tensor_sub(out=bias_out, in0=shift, in1=rstd[:])
 
 
 def tile_settransform_pa_t_kernel(
@@ -98,15 +98,15 @@ def tile_settransform_pa_t_kernel(
 
         with tc.tile_pool(name="early", bufs=1) as early, tc.tile_pool(
             name="xin", bufs=PASSES * CHUNKS
-        ) as xin, tc.tile_pool(name="stage", bufs=5) as stage, tc.tile_pool(
+        ) as xin, tc.tile_pool(name="stage", bufs=8) as stage, tc.tile_pool(
             name="words", bufs=3
         ) as words:
-            stats0 = early.tile([P, PASSES, PACK, BN_CHUNKS, 6], F32)
-            moments0 = early.tile([P, PASSES, PACK, 2], F32)
-            squares0 = early.tile([P, PASSES, PACK], F32)
-            mean0 = early.tile([P, PASSES, PACK], F32)
-            part0 = early.tile([P, PASSES, 2, PACK], F32)
-            var0 = early.tile([P, PASSES, PACK], F32)
+            stats0 = early.tile([P, HALVES, len(BN_CHUNKS), 2, 6], F32)
+            moments0 = early.tile([P, PACK, 2], F32)
+            natural = early.tile([P, PASSES, K_BLOCKS, 2], F32)
+            spread = early.tile([P, PASSES, K_BLOCKS * 2, PACK], F32)
+            part0 = early.tile([P, 2, PACK], F32)
+            total0 = early.tile([P, PASSES, 2, PACK], F32)
             scale0 = early.tile([P, PASSES, PACK], F32)
             bias0 = early.tile([P, PASSES, PACK], F32)
             product = early.tile([P, P], F32)
@@ -114,13 +114,10 @@ def tile_settransform_pa_t_kernel(
             x_tiles = {}
             for g in range(PASSES):
                 for c in range(CHUNKS):
-                    x_sb = xin.tile([P, ROW_TILES, K_PASS + PAD], BF16, name="x_sb")
+                    x_sb = xin.tile([P, ROW_TILES, K_PASS], BF16, name="x_sb")
                     x_tiles[(g, c)] = x_sb
-                    if c >= BN_CHUNKS:
-                        nc.gpsimd.memset(x_sb[:, :, K_PASS:], 1.0)
                     nc.sync.dma_start(
-                        out=x_sb[:, :, 0:K_PASS],
-                        in_=x_view[c][:, :, g * K_PASS : (g + 1) * K_PASS],
+                        out=x_sb[:], in_=x_view[c][:, :, g * K_PASS : (g + 1) * K_PASS]
                     )
             for g in range(PASSES):
                 nc.sync.dma_start(
@@ -134,43 +131,75 @@ def tile_settransform_pa_t_kernel(
                         in_=W0_scales[g, 4 * q : 4 * q + 4, :].bitcast(I32),
                     )
 
-            def turn(g, a, t, i):
-                x_ps = bank(i, [P, PIECE], BF16)
-                for k in range(PIECE // P):
-                    c, j = divmod(a * (PIECE // P) + k, ROW_TILES)
+            ones = early.tile([P, 2], BF16)
+            nc.vector.memset(ones[:], 1.0)
+            slot = early.tile([P, PACK], F32)
+            nc.vector.tensor_reduce(
+                out=slot[:],
+                in_=ident_f32[:].rearrange("p (i t) -> p t i", t=PACK),
+                axis=AXIS.X,
+                op=ALU.add,
+            )
+            nc.vector.tensor_scalar(
+                out=slot[:], in0=slot[:], scalar1=1.0 / ROWS, scalar2=0.0, op0=ALU.mult, op1=ALU.add
+            )
+            home = early.tile([P, K_BLOCKS, P // K_BLOCKS], F32)
+            for b in range(K_BLOCKS):
+                nc.vector.tensor_reduce(
+                    out=home[:, b, :],
+                    in_=ident_f32[:].rearrange("p (i t) -> p i t", t=PACK),
+                    axis=AXIS.X,
+                    op=ALU.add,
+                )
+            here = early.tile([P, K_BLOCKS], F32)
+            nc.vector.tensor_reduce(
+                out=here[:],
+                in_=ident_f32[:].rearrange("p (b i) -> p b i", b=K_BLOCKS),
+                axis=AXIS.X,
+                op=ALU.add,
+            )
+
+            turns = []
+
+            def turn(g, c, u):
+                x_ps = bank(len(turns) % WORD_BANKS, [P, CHUNK], F32)
+                turns.append((g, c, u))
+                for j in range(ROW_TILES):
                     nc.tensor.transpose(
-                        out=x_ps[:, k * P : (k + 1) * P],
-                        in_=x_tiles[(g, c)][:, j, t:K_PASS:PACK],
-                        identity=ident_bf16[:],
+                        out=x_ps[:, j * P : (j + 1) * P],
+                        in_=x_tiles[(g, c)][:, j, :].bitcast(F32)[:, u : K_PASS // 2 : HALVES],
+                        identity=ident_f32[:],
                     )
                 return x_ps
 
-            def bank_statistics(g, t, x_ps):
-                for s in range(BN_CHUNKS):
-                    nc.vector.bn_stats(
-                        out=stats0[:, g, t, s, :], in_=x_ps[:, s:PIECE:BN_CHUNKS]
-                    )
+            def chunk_statistics(c):
+                for u in range(HALVES):
+                    pairs = turn(0, c, u)[:].bitcast(BF16)
+                    for s in range(2):
+                        nc.vector.bn_stats(
+                            out=stats0[:, u, BN_CHUNKS.index(c), s, :],
+                            in_=pairs[:, s * BN_MAX : (s + 1) * BN_MAX],
+                        )
 
-            def first_part(g):
-                for t in range(PACK):
-                    nc.vector.bn_aggr(
-                        out=moments0[:, g, t, :],
-                        in_=stats0[:, g, t, :, :].rearrange("p s (h v) -> p (s h) v", v=3),
-                    )
-                share = BN_CHUNKS / CHUNKS
-                mean, var = moments0[:, g, :, 0], moments0[:, g, :, 1]
-                nc.gpsimd.tensor_mul(out=part0[:, g, 1, :], in0=mean, in1=mean)
-                nc.gpsimd.tensor_add(out=part0[:, g, 1, :], in0=part0[:, g, 1, :], in1=var)
+            def first_part():
+                for u in range(HALVES):
+                    for e in range(2):
+                        nc.vector.bn_aggr(
+                            out=moments0[:, 2 * u + e, :],
+                            in_=stats0[:, u, :, :, 3 * e : 3 * e + 3].rearrange(
+                                "p c s v -> p (c s) v"
+                            ),
+                        )
+                share = len(BN_CHUNKS) / CHUNKS
+                mean, var = moments0[:, :, 0], moments0[:, :, 1]
+                square = part0[:, 0, :]
+                nc.gpsimd.tensor_mul(out=square, in0=mean, in1=mean)
+                nc.gpsimd.tensor_add(out=square, in0=square, in1=var)
                 nc.gpsimd.tensor_scalar(
-                    out=part0[:, g, 1, :],
-                    in0=part0[:, g, 1, :],
-                    scalar1=share,
-                    scalar2=0.0,
-                    op0=ALU.mult,
-                    op1=ALU.add,
+                    out=square, in0=square, scalar1=share, scalar2=0.0, op0=ALU.mult, op1=ALU.add
                 )
                 nc.gpsimd.tensor_scalar(
-                    out=part0[:, g, 0, :],
+                    out=part0[:, 1, :],
                     in0=mean,
                     scalar1=share,
                     scalar2=0.0,
@@ -178,45 +207,96 @@ def tile_settransform_pa_t_kernel(
                     op1=ALU.add,
                 )
 
-            def sums(g, c, j, grams):
-                x_sb = x_tiles[(g, c)]
-                for t in range(PACK):
+            def open_sums(g):
+                squares = [bank(BANKS + b, [P, CHUNK], F32) for b in range(K_BLOCKS)]
+                return squares, bank(SUM_BANK, [P, CHUNK], F32)
+
+            def add_sums(g, c, b, banks):
+                squares, sums = banks
+                chunks = SUM_CHUNKS[g]
+                column = b * CHUNKS + chunks.index(c)
+                for j in range(ROW_TILES):
+                    rows = x_tiles[(g, c)][:, j, b * P : (b + 1) * P]
                     nc.tensor.matmul(
-                        out=grams[t][:, 0:GRAM_COLS],
-                        lhsT=x_sb[:, j, t:K_PASS:PACK],
-                        rhs=x_sb[:, j, t : K_PASS + t + 1 : PACK],
-                        start=(c == BN_CHUNKS and j == 0),
-                        stop=(c == CHUNKS - 1 and j == ROW_TILES - 1),
+                        out=squares[b][:, 0:P],
+                        lhsT=rows,
+                        rhs=rows,
+                        start=(c == chunks[0] and j == 0),
+                        stop=(c == chunks[-1] and j == ROW_TILES - 1),
+                    )
+                    nc.tensor.matmul(
+                        out=sums[:, column : column + 1],
+                        lhsT=rows,
+                        rhs=ones[:, 0:1],
+                        start=(j == 0),
+                        stop=(j == ROW_TILES - 1),
                     )
 
-            def coefficients(g, grams):
-                for t in range(PACK):
+            def read_sums(g, banks):
+                squares, sums = banks
+                for b in range(K_BLOCKS):
                     nc.vector.scalar_tensor_tensor(
                         out=product[:],
-                        in0=grams[t][:, 0:P],
-                        scalar=1.0 / ROWS,
+                        in0=squares[b][:, 0:P],
+                        scalar=1.0,
                         in1=ident_f32[:],
                         op0=ALU.mult,
                         op1=ALU.mult,
-                        accum_out=squares0[:, g, t : t + 1],
+                        accum_out=natural[:, g, b, 0:1],
                     )
-                    nc.vector.scalar_tensor_tensor(
-                        out=mean0[:, g, t : t + 1],
-                        in0=grams[t][:, P:GRAM_COLS],
-                        scalar=1.0 / ROWS,
-                        in1=part0[:, g, 0, t : t + 1],
-                        op0=ALU.mult,
-                        op1=ALU.add,
+                nc.vector.tensor_reduce(
+                    out=natural[:, g, :, 1],
+                    in_=sums[:, 0 : K_BLOCKS * CHUNKS].rearrange("p (b c) -> p b c", c=CHUNKS)[
+                        :, :, 0 : len(SUM_CHUNKS[g])
+                    ],
+                    axis=AXIS.X,
+                    op=ALU.add,
+                )
+                nc.vector.tensor_mul(
+                    out=spread[:, g, :, :],
+                    in0=natural[:, g, :, :]
+                    .rearrange("p b v -> p (b v)")
+                    .unsqueeze(2)
+                    .to_broadcast([P, K_BLOCKS * 2, PACK]),
+                    in1=slot[:].unsqueeze(1).to_broadcast([P, K_BLOCKS * 2, PACK]),
+                )
+
+            def coefficients(g, engine):
+                packed = bank(len(turns) % WORD_BANKS, [P, CHUNK], F32)
+                turns.append("packed")
+                nc.tensor.matmul(
+                    out=packed[:, 0 : K_BLOCKS * 2 * PACK],
+                    lhsT=home[:].rearrange("p b i -> p (b i)"),
+                    rhs=spread[:, g, :, :].rearrange("p m t -> p (m t)"),
+                    start=True,
+                    stop=True,
+                )
+                nc.vector.tensor_mul(
+                    out=spread[:, g, :, :].rearrange("p (b v) t -> p b (v t)", v=2),
+                    in0=packed[:, 0 : K_BLOCKS * 2 * PACK].rearrange("p (b m) -> p b m", b=K_BLOCKS),
+                    in1=here[:].unsqueeze(2).to_broadcast([P, K_BLOCKS, 2 * PACK]),
+                )
+                nc.vector.tensor_reduce(
+                    out=total0[:, g, :, :].rearrange("p v t -> p (v t)"),
+                    in_=spread[:, g, :, :].rearrange("p (b v) t -> p (v t) b", v=2),
+                    axis=AXIS.X,
+                    op=ALU.add,
+                )
+                if g == 0:
+                    engine.tensor_add(
+                        out=total0[:, g, :, :], in0=total0[:, g, :, :], in1=part0[:]
                     )
-                nc.vector.tensor_add(out=var0[:, g, :], in0=squares0[:, g, :], in1=part0[:, g, 1, :])
-                nc.vector.tensor_mul(out=part0[:, g, 0, :], in0=mean0[:, g, :], in1=mean0[:, g, :])
-                nc.vector.tensor_sub(out=var0[:, g, :], in0=var0[:, g, :], in1=part0[:, g, 0, :])
+                mean, var = total0[:, g, 1, :], total0[:, g, 0, :]
+                square = small.tile([P, PACK], F32)
+                engine.tensor_mul(out=square[:], in0=mean, in1=mean)
+                engine.tensor_sub(out=var, in0=var, in1=square[:])
                 norm_coefficients(
                     nc,
+                    engine,
                     small,
                     neg_half,
-                    mean0[:, g, :],
-                    var0[:, g, :],
+                    mean,
+                    var,
                     gain0[:, g, :],
                     shift0[:, g, :],
                     scale0[:, g, :],
@@ -225,27 +305,30 @@ def tile_settransform_pa_t_kernel(
 
             planes_tiles = {}
 
-            def affine(g, a, t, x_ps, on_vector=False):
-                if (g, a) not in planes_tiles:
-                    planes_tiles[(g, a)] = stage.tile([P, PACK, PIECE], BF16, name="planes")
-                out_plane = planes_tiles[(g, a)][:, t, :]
-                if on_vector:
-                    nc.vector.tensor_scalar(
-                        out=out_plane,
-                        in0=x_ps[:],
-                        scalar1=scale0[:, g, t : t + 1],
-                        scalar2=bias0[:, g, t : t + 1],
-                        op0=ALU.mult,
-                        op1=ALU.add,
-                    )
-                else:
-                    nc.scalar.activation(
-                        out=out_plane,
-                        in_=x_ps[:],
-                        func=ACT.Identity,
-                        scale=scale0[:, g, t : t + 1],
-                        bias=bias0[:, g, t : t + 1],
-                    )
+            def affine(g, c, u, x_ps):
+                if (g, c) not in planes_tiles:
+                    planes_tiles[(g, c)] = stage.tile([P, PACK, CHUNK], BF16, name="planes")
+                for e in range(2):
+                    t = 2 * u + e
+                    out_plane = planes_tiles[(g, c)][:, t, :]
+                    column = x_ps[:].bitcast(BF16)[:, e : 2 * CHUNK : 2]
+                    if (t == PACK - 1 and c % 2 == 1) or (g == 0 and c == 0 and u == 1):
+                        nc.vector.tensor_scalar(
+                            out=out_plane,
+                            in0=column,
+                            scalar1=scale0[:, g, t : t + 1],
+                            scalar2=bias0[:, g, t : t + 1],
+                            op0=ALU.mult,
+                            op1=ALU.add,
+                        )
+                    else:
+                        nc.scalar.activation(
+                            out=out_plane,
+                            in_=column,
+                            func=ACT.Identity,
+                            scale=scale0[:, g, t : t + 1],
+                            bias=bias0[:, g, t : t + 1],
+                        )
 
             waiting = []
 
@@ -259,62 +342,58 @@ def tile_settransform_pa_t_kernel(
                 )
 
             def group(g, c):
-                a, s = divmod(c, PIECE // CHUNK)
                 grouped = words.tile([P, CHUNK, PACK], BF16, align_bytes=64)
                 nc.vector.tensor_copy(
                     out=grouped[:].rearrange("p (c i) t -> p c t i", i=4),
-                    in_=planes_tiles[(g, a)][:, :, s * CHUNK : (s + 1) * CHUNK].rearrange(
-                        "p t (c i) -> p c t i", i=4
-                    ),
+                    in_=planes_tiles[(g, c)][:].rearrange("p t (c i) -> p c t i", i=4),
                 )
                 if waiting:
                     quantise()
                 waiting.append((g, slice(c * CHUNK, (c + 1) * CHUNK), grouped))
 
-            held = {}
-            for t in range(PACK):
-                held[t] = turn(0, 0, t, t)
-                bank_statistics(0, t, held[t])
-            first_part(0)
-            grams0 = [bank(BANKS + t, [P, CHUNK], F32) for t in range(PACK)]
-            for c in range(BN_CHUNKS, CHUNKS):
-                for j in range(ROW_TILES):
-                    sums(0, c, j, grams0)
-            coefficients(0, grams0)
+            banks0 = open_sums(0)
+            for c in range(CHUNKS):
+                if c in BN_CHUNKS:
+                    chunk_statistics(c)
+                else:
+                    for b in range(K_BLOCKS):
+                        add_sums(0, c, b, banks0)
+            first_part()
+            read_sums(0, banks0)
+            ready = [(0, 0, u, turn(0, 0, u)) for u in range(HALVES)]
+            coefficients(0, nc.vector)
 
-            for t in range(PACK):
-                bank_statistics(1, t, turn(1, 0, t, BANKS + t))
-            first_part(1)
+            banks1 = open_sums(1)
+            units = [(c, b) for c in range(CHUNKS) for b in range(K_BLOCKS)]
+            for c, b in units[:AHEAD]:
+                add_sums(1, c, b, banks1)
+            fills = [(c, u) for c in range(CHUNKS) for u in range(HALVES)]
+            for n, (c, u) in enumerate(fills):
+                if n >= len(ready):
+                    x_ps = turn(0, c, u)
+                    lo = AHEAD + 2 * (n - len(ready))
+                    for c1, b1 in units[lo : lo + 2]:
+                        add_sums(1, c1, b1, banks1)
+                else:
+                    x_ps = ready[n][3]
+                affine(0, c, u, x_ps)
+                if (c, u) == (4, 0):
+                    read_sums(1, banks1)
+                if (c, u) == (6, 0):
+                    coefficients(1, nc.gpsimd)
+                if u == HALVES - 1 and c >= 1:
+                    group(0, c - 1)
+            group(0, CHUNKS - 1)
 
-            for t in range(PACK):
-                affine(0, 0, t, held[t])
-            for t in range(PACK):
-                affine(0, 1, t, turn(0, 1, t, t))
-            grams1 = [bank(BANKS + t, [P, CHUNK], F32) for t in range(PACK)]
-            row_tiles = [(c, j) for c in range(BN_CHUNKS, CHUNKS) for j in range(ROW_TILES)]
-            share = len(row_tiles) // (2 * PACK)
-            for n in range(2 * PACK):
-                for c, j in row_tiles[n * share : (n + 1) * share]:
-                    sums(1, c, j, grams1)
-                a, t = 2 + n // PACK, n % PACK
-                affine(0, a, t, turn(0, a, t, t))
-            for c in range(6):
-                group(0, c)
-            coefficients(1, grams1)
-            for c in range(6, CHUNKS):
-                group(0, c)
-
-            for a in range(PIECES):
-                for t in range(PACK):
-                    x_ps = turn(1, a, t, (a % 2) * BANKS + t)
-                    affine(1, a, t, x_ps, t == VECTOR_PLANE)
-                for c in (2 * a, 2 * a + 1):
-                    group(1, c)
-            quantise()
-
-            params_ps = bank(BANKS, [P, PIECE], BF16)
+            params_ps = bank(BANKS, [P, 2 * CHUNK], BF16)
             nc.tensor.transpose(out=params_ps[:, 0:P], in_=param_rows[:], identity=ident_bf16[:])
             nc.vector.tensor_copy(out=params[:], in_=params_ps[:, 0 : 3 * BLOCKS])
+
+            for c, u in fills:
+                affine(1, c, u, turn(1, c, u))
+                if u == HALVES - 1:
+                    group(1, c)
+            quantise()
 
         with tc.tile_pool(name="hidden", bufs=3) as hidden, tc.tile_pool(
             name="outs", bufs=8
@@ -358,6 +437,7 @@ def tile_settransform_pa_t_kernel(
                 bias1 = small.tile([P, 1], F32)
                 norm_coefficients(
                     nc,
+                    nc.gpsimd,
                     small,
                     neg_half,
                     moments1[:, 0:1],

@@ -22,33 +22,25 @@ CHUNK = 512
 CHUNKS = ROWS // CHUNK
 ROW_TILES = CHUNK // P
 BLOCKS = D_OUT // P
-HALVES = 2
-BN_MAX = 512
-BN_CHUNKS = (0, 1, 2, 4)
-SUM_CHUNKS = ((3, 5, 6, 7), tuple(range(CHUNKS)))
 K_BLOCKS = K_PASS // P
+HALVES = 2
+X_TILES = 13
+BN_CHUNKS = ((0, 1, 2, 4), (0,))
+SUM_CHUNKS = tuple(tuple(c for c in range(CHUNKS) if c not in bn) for bn in BN_CHUNKS)
+RAW = (0, 1, 2, 4, 3, 5)
+ORDER = RAW + (6, 7)
+SCALAR_GROUPS = (1, 4, 5)
 WORD_BANKS = 3
 SUM_BANK = 3
 BANKS = 4
-AHEAD = 20
 NORM_COLS = 1024
 RUN = 4
 LAG = 3
+TAIL = 4
+V_COPIES = (0, 2, 4, 6)
 EPS = 1e-5
 
 FLOPS = 2 * ROWS * D_IN * D_OUT
-
-
-def norm_coefficients(nc, engine, pool, neg_half, mean, var, gain, shift, scale_out, bias_out):
-    width = scale_out.shape[1]
-    rstd = pool.tile([P, width], F32)
-    engine.tensor_scalar(
-        out=rstd[:], in0=var, scalar1=0.0, scalar2=EPS, op0=ALU.max, op1=ALU.add
-    )
-    nc.gpsimd.tensor_tensor(out=rstd[:], in0=rstd[:], in1=neg_half[:, 0:width], op=ALU.pow)
-    engine.tensor_mul(out=scale_out, in0=gain, in1=rstd[:])
-    engine.tensor_mul(out=rstd[:], in0=mean, in1=scale_out)
-    engine.tensor_sub(out=bias_out, in0=shift, in1=rstd[:])
 
 
 def tile_settransform_pa_t_kernel(
@@ -96,17 +88,33 @@ def tile_settransform_pa_t_kernel(
         x_scales = keep.tile([P, PASSES, ROWS], U8, align_bytes=64)
         params = keep.tile([P, 3 * BLOCKS], F32)
 
+        def inverse_root(pool, engine, var):
+            rstd = pool.tile([P, var.shape[1]], F32, name="rstd")
+            engine.tensor_scalar(
+                out=rstd[:], in0=var, scalar1=0.0, scalar2=EPS, op0=ALU.max, op1=ALU.add
+            )
+            nc.gpsimd.tensor_tensor(
+                out=rstd[:], in0=rstd[:], in1=neg_half[:, 0 : var.shape[1]], op=ALU.pow
+            )
+            return rstd
+
+        def scale_and_bias(engine, mean, rstd, gain, shift, scale_out, bias_out):
+            engine.tensor_mul(out=scale_out, in0=gain, in1=rstd[:])
+            engine.tensor_mul(out=rstd[:], in0=mean, in1=scale_out)
+            engine.tensor_sub(out=bias_out, in0=shift, in1=rstd[:])
+
         with tc.tile_pool(name="early", bufs=1) as early, tc.tile_pool(
-            name="xin", bufs=PASSES * CHUNKS
-        ) as xin, tc.tile_pool(name="stage", bufs=8) as stage, tc.tile_pool(
+            name="xin", bufs=X_TILES
+        ) as xin, tc.tile_pool(name="stage", bufs=11) as stage, tc.tile_pool(
             name="words", bufs=3
-        ) as words:
-            stats0 = early.tile([P, HALVES, len(BN_CHUNKS), 2, 6], F32)
-            moments0 = early.tile([P, PACK, 2], F32)
+        ) as words, tc.tile_pool(name="scalar_words", bufs=2) as scalar_words:
+            stats0 = early.tile([P, PASSES, PACK, len(BN_CHUNKS[0]), 6], F32)
+            moments0 = early.tile([P, PASSES, PACK, 2], F32)
             natural = early.tile([P, PASSES, K_BLOCKS, 2], F32)
             spread = early.tile([P, PASSES, K_BLOCKS * 2, PACK], F32)
-            part0 = early.tile([P, 2, PACK], F32)
+            part0 = early.tile([P, PASSES, 2, PACK], F32)
             total0 = early.tile([P, PASSES, 2, PACK], F32)
+            square0 = early.tile([P, PASSES, PACK], F32)
             scale0 = early.tile([P, PASSES, PACK], F32)
             bias0 = early.tile([P, PASSES, PACK], F32)
             product = early.tile([P, P], F32)
@@ -160,54 +168,57 @@ def tile_settransform_pa_t_kernel(
             )
 
             turns = []
+            planes_tiles = {}
+            grouped_tiles = {}
+            word_tiles = {}
 
             def turn(g, c, u):
                 x_ps = bank(len(turns) % WORD_BANKS, [P, CHUNK], F32)
                 turns.append((g, c, u))
+                word_tiles[(g, c, u)] = x_ps
                 for j in range(ROW_TILES):
                     nc.tensor.transpose(
                         out=x_ps[:, j * P : (j + 1) * P],
                         in_=x_tiles[(g, c)][:, j, :].bitcast(F32)[:, u : K_PASS // 2 : HALVES],
                         identity=ident_f32[:],
                     )
-                return x_ps
 
-            def chunk_statistics(c):
-                for u in range(HALVES):
-                    pairs = turn(0, c, u)[:].bitcast(BF16)
-                    for s in range(2):
-                        nc.vector.bn_stats(
-                            out=stats0[:, u, BN_CHUNKS.index(c), s, :],
-                            in_=pairs[:, s * BN_MAX : (s + 1) * BN_MAX],
-                        )
+            def planes_of(g, c):
+                if (g, c) not in planes_tiles:
+                    planes_tiles[(g, c)] = stage.tile([P, PACK, CHUNK], BF16, name="planes")
+                return planes_tiles[(g, c)]
 
-            def first_part():
-                for u in range(HALVES):
-                    for e in range(2):
-                        nc.vector.bn_aggr(
-                            out=moments0[:, 2 * u + e, :],
-                            in_=stats0[:, u, :, :, 3 * e : 3 * e + 3].rearrange(
-                                "p c s v -> p (c s) v"
-                            ),
-                        )
-                share = len(BN_CHUNKS) / CHUNKS
-                mean, var = moments0[:, :, 0], moments0[:, :, 1]
-                square = part0[:, 0, :]
+            def feature(g, c, t):
+                u, e = divmod(t, 2)
+                return word_tiles[(g, c, u)][:].bitcast(BF16)[:, e : 2 * CHUNK : 2]
+
+            def raw_planes(g, c, u):
+                for t in (2 * u, 2 * u + 1):
+                    nc.scalar.copy(out=planes_of(g, c)[:, t, :], in_=feature(g, c, t))
+
+            def plane_statistics(g, c, t):
+                nc.vector.bn_stats(
+                    out=stats0[:, g, t, BN_CHUNKS[g].index(c), :], in_=planes_of(g, c)[:, t, :]
+                )
+
+            def first_part(g):
+                count = len(BN_CHUNKS[g])
+                for t in range(PACK):
+                    nc.vector.bn_aggr(
+                        out=moments0[:, g, t, :],
+                        in_=stats0[:, g, t, 0:count, :].rearrange("p c (s v) -> p (c s) v", v=3),
+                    )
+                share = count / CHUNKS
+                mean, var = moments0[:, g, :, 0], moments0[:, g, :, 1]
+                square = part0[:, g, 0, :]
                 nc.gpsimd.tensor_mul(out=square, in0=mean, in1=mean)
                 nc.gpsimd.tensor_add(out=square, in0=square, in1=var)
-                nc.gpsimd.tensor_scalar(
-                    out=square, in0=square, scalar1=share, scalar2=0.0, op0=ALU.mult, op1=ALU.add
-                )
-                nc.gpsimd.tensor_scalar(
-                    out=part0[:, 1, :],
-                    in0=mean,
-                    scalar1=share,
-                    scalar2=0.0,
-                    op0=ALU.mult,
-                    op1=ALU.add,
-                )
+                for value, out_part in ((square, square), (mean, part0[:, g, 1, :])):
+                    nc.gpsimd.tensor_scalar(
+                        out=out_part, in0=value, scalar1=share, scalar2=0.0, op0=ALU.mult, op1=ALU.add
+                    )
 
-            def open_sums(g):
+            def open_sums():
                 squares = [bank(BANKS + b, [P, CHUNK], F32) for b in range(K_BLOCKS)]
                 return squares, bank(SUM_BANK, [P, CHUNK], F32)
 
@@ -261,9 +272,10 @@ def tile_settransform_pa_t_kernel(
                     in1=slot[:].unsqueeze(1).to_broadcast([P, K_BLOCKS * 2, PACK]),
                 )
 
-            def coefficients(g, engine):
+            def pack_sums(g):
                 packed = bank(len(turns) % WORD_BANKS, [P, CHUNK], F32)
                 turns.append("packed")
+                word_tiles[(g, "packed")] = packed
                 nc.tensor.matmul(
                     out=packed[:, 0 : K_BLOCKS * 2 * PACK],
                     lhsT=home[:].rearrange("p b i -> p (b i)"),
@@ -271,9 +283,13 @@ def tile_settransform_pa_t_kernel(
                     start=True,
                     stop=True,
                 )
+
+            def root_of(g):
                 nc.vector.tensor_mul(
                     out=spread[:, g, :, :].rearrange("p (b v) t -> p b (v t)", v=2),
-                    in0=packed[:, 0 : K_BLOCKS * 2 * PACK].rearrange("p (b m) -> p b m", b=K_BLOCKS),
+                    in0=word_tiles[(g, "packed")][:, 0 : K_BLOCKS * 2 * PACK].rearrange(
+                        "p (b m) -> p b m", b=K_BLOCKS
+                    ),
                     in1=here[:].unsqueeze(2).to_broadcast([P, K_BLOCKS, 2 * PACK]),
                 )
                 nc.vector.tensor_reduce(
@@ -282,120 +298,163 @@ def tile_settransform_pa_t_kernel(
                     axis=AXIS.X,
                     op=ALU.add,
                 )
-                if g == 0:
-                    engine.tensor_add(
-                        out=total0[:, g, :, :], in0=total0[:, g, :, :], in1=part0[:]
-                    )
+                nc.vector.tensor_add(
+                    out=total0[:, g, :, :], in0=total0[:, g, :, :], in1=part0[:, g, :, :]
+                )
                 mean, var = total0[:, g, 1, :], total0[:, g, 0, :]
-                square = small.tile([P, PACK], F32)
-                engine.tensor_mul(out=square[:], in0=mean, in1=mean)
-                engine.tensor_sub(out=var, in0=var, in1=square[:])
-                norm_coefficients(
-                    nc,
-                    engine,
-                    small,
-                    neg_half,
-                    mean,
-                    var,
+                nc.vector.tensor_mul(out=square0[:, g, :], in0=mean, in1=mean)
+                nc.vector.tensor_sub(out=var, in0=var, in1=square0[:, g, :])
+                return inverse_root(early, nc.vector, var)
+
+            def coefficients(g, rstd):
+                scale_and_bias(
+                    nc.vector,
+                    total0[:, g, 1, :],
+                    rstd,
                     gain0[:, g, :],
                     shift0[:, g, :],
                     scale0[:, g, :],
                     bias0[:, g, :],
                 )
 
-            planes_tiles = {}
+            def affine_planes(g, c):
+                for t in range(PACK):
+                    plane = planes_of(g, c)[:, t, :]
+                    nc.vector.tensor_scalar(
+                        out=plane,
+                        in0=plane,
+                        scalar1=scale0[:, g, t : t + 1],
+                        scalar2=bias0[:, g, t : t + 1],
+                        op0=ALU.mult,
+                        op1=ALU.add,
+                    )
 
-            def affine(g, c, u, x_ps):
-                if (g, c) not in planes_tiles:
-                    planes_tiles[(g, c)] = stage.tile([P, PACK, CHUNK], BF16, name="planes")
-                for e in range(2):
-                    t = 2 * u + e
-                    out_plane = planes_tiles[(g, c)][:, t, :]
-                    column = x_ps[:].bitcast(BF16)[:, e : 2 * CHUNK : 2]
-                    if (t == PACK - 1 and c % 2 == 1) or (g == 0 and c == 0 and u == 1):
-                        nc.vector.tensor_scalar(
-                            out=out_plane,
-                            in0=column,
-                            scalar1=scale0[:, g, t : t + 1],
-                            scalar2=bias0[:, g, t : t + 1],
-                            op0=ALU.mult,
-                            op1=ALU.add,
-                        )
-                    else:
-                        nc.scalar.activation(
-                            out=out_plane,
-                            in_=column,
-                            func=ACT.Identity,
-                            scale=scale0[:, g, t : t + 1],
-                            bias=bias0[:, g, t : t + 1],
-                        )
+            def affine_bank(g, c, u):
+                for t in (2 * u, 2 * u + 1):
+                    nc.scalar.activation(
+                        out=planes_of(g, c)[:, t, :],
+                        in_=feature(g, c, t),
+                        func=ACT.Identity,
+                        scale=scale0[:, g, t : t + 1],
+                        bias=bias0[:, g, t : t + 1],
+                    )
 
-            waiting = []
-
-            def quantise():
-                g, cols, grouped = waiting[0]
-                waiting.clear()
+            def quantise(g, c):
+                cols = slice(c * CHUNK, (c + 1) * CHUNK)
                 nc.vector.quantize_mx(
                     out=x_codes[:, g, cols].bitcast(FP8X4),
                     scales=x_scales[:, g, cols],
-                    in_=grouped[:].rearrange("p c t -> p (c t)"),
+                    in_=grouped_tiles[(g, c)][:].rearrange("p c t -> p (c t)"),
                 )
 
-            def group(g, c):
-                grouped = words.tile([P, CHUNK, PACK], BF16, align_bytes=64)
-                nc.vector.tensor_copy(
-                    out=grouped[:].rearrange("p (c i) t -> p c t i", i=4),
-                    in_=planes_tiles[(g, c)][:].rearrange("p t (c i) -> p c t i", i=4),
-                )
-                if waiting:
-                    quantise()
-                waiting.append((g, slice(c * CHUNK, (c + 1) * CHUNK), grouped))
+            def group(g, c, on_scalar):
+                if on_scalar:
+                    grouped = scalar_words.tile([P, CHUNK, PACK], BF16, align_bytes=64)
+                    nc.scalar.copy(
+                        out=grouped[:], in_=planes_of(g, c)[:].rearrange("p t c -> p c t")
+                    )
+                else:
+                    grouped = words.tile([P, CHUNK, PACK], BF16, align_bytes=64)
+                    nc.vector.tensor_copy(
+                        out=grouped[:].rearrange("p (c i) t -> p c t i", i=4),
+                        in_=planes_of(g, c)[:].rearrange("p t (c i) -> p c t i", i=4),
+                    )
+                grouped_tiles[(g, c)] = grouped
 
-            banks0 = open_sums(0)
+            banks0 = open_sums()
             for c in range(CHUNKS):
-                if c in BN_CHUNKS:
-                    chunk_statistics(c)
+                if c in BN_CHUNKS[0]:
+                    for u in range(HALVES):
+                        turn(0, c, u)
+                        raw_planes(0, c, u)
+                        for t in (2 * u, 2 * u + 1):
+                            plane_statistics(0, c, t)
                 else:
                     for b in range(K_BLOCKS):
                         add_sums(0, c, b, banks0)
-            first_part()
+            first_part(0)
             read_sums(0, banks0)
-            ready = [(0, 0, u, turn(0, 0, u)) for u in range(HALVES)]
-            coefficients(0, nc.vector)
+            banks1 = open_sums()
+            left = [(c, b) for c in SUM_CHUNKS[1] for b in range(K_BLOCKS)]
 
-            banks1 = open_sums(1)
-            units = [(c, b) for c in range(CHUNKS) for b in range(K_BLOCKS)]
-            for c, b in units[:AHEAD]:
-                add_sums(1, c, b, banks1)
-            fills = [(c, u) for c in range(CHUNKS) for u in range(HALVES)]
-            for n, (c, u) in enumerate(fills):
-                if n >= len(ready):
-                    x_ps = turn(0, c, u)
-                    lo = AHEAD + 2 * (n - len(ready))
-                    for c1, b1 in units[lo : lo + 2]:
-                        add_sums(1, c1, b1, banks1)
-                else:
-                    x_ps = ready[n][3]
-                affine(0, c, u, x_ps)
-                if (c, u) == (4, 0):
-                    read_sums(1, banks1)
-                if (c, u) == (6, 0):
-                    coefficients(1, nc.gpsimd)
-                if u == HALVES - 1 and c >= 1:
-                    group(0, c - 1)
-            group(0, CHUNKS - 1)
+            def sums1(lo, hi):
+                for c, b in left[lo:hi]:
+                    add_sums(1, c, b, banks1)
 
-            params_ps = bank(BANKS, [P, 2 * CHUNK], BF16)
+            turn(1, 0, 0)
+            turn(1, 0, 1)
+            sums1(0, 4)
+            pack_sums(0)
+            raw_planes(1, 0, 0)
+            raw_planes(1, 0, 1)
+            plane_statistics(1, 0, 0)
+            rstd0 = root_of(0)
+            turn(0, 3, 0)
+            turn(0, 3, 1)
+            raw_planes(0, 3, 0)
+            raw_planes(0, 3, 1)
+            plane_statistics(1, 0, 1)
+            plane_statistics(1, 0, 2)
+            coefficients(0, rstd0)
+            sums1(4, 12)
+            turn(0, 5, 0)
+            turn(0, 5, 1)
+            raw_planes(0, 5, 0)
+            raw_planes(0, 5, 1)
+            sums1(12, 16)
+            sums1(16, len(left))
+            turn(0, 6, 0)
+            turn(0, 6, 1)
+            affine_planes(0, 0)
+            affine_planes(0, 1)
+            group(0, 0, False)
+            group(0, 1, True)
+            affine_planes(0, 2)
+            affine_planes(0, 4)
+            group(0, 2, False)
+            group(0, 4, True)
+            quantise(0, 0)
+            affine_planes(0, 3)
+            affine_bank(0, 6, 0)
+            affine_bank(0, 6, 1)
+            quantise(0, 1)
+            plane_statistics(1, 0, 3)
+            first_part(1)
+            read_sums(1, banks1)
+            pack_sums(1)
+            turn(0, 7, 0)
+            turn(0, 7, 1)
+            group(0, 3, False)
+            rstd1 = root_of(1)
+            affine_bank(0, 7, 0)
+            affine_bank(0, 7, 1)
+            affine_planes(0, 5)
+            quantise(0, 2)
+            quantise(0, 4)
+            coefficients(1, rstd1)
+            group(0, 5, True)
+            affine_planes(1, 0)
+            group(0, 6, False)
+            quantise(0, 3)
+            group(0, 7, False)
+            quantise(0, 6)
+            group(1, 0, False)
+            quantise(0, 7)
+            quantise(0, 5)
+
+            params_ps = bank(SUM_BANK, [P, 2 * CHUNK], BF16)
             nc.tensor.transpose(out=params_ps[:, 0:P], in_=param_rows[:], identity=ident_bf16[:])
             nc.vector.tensor_copy(out=params[:], in_=params_ps[:, 0 : 3 * BLOCKS])
 
-            for c, u in fills:
-                affine(1, c, u, turn(1, c, u))
-                if u == HALVES - 1:
-                    group(1, c)
-            quantise()
+            for c in range(1, CHUNKS):
+                for u in range(HALVES):
+                    turn(1, c, u)
+                    affine_bank(1, c, u)
+                group(1, c, False)
+                quantise(1, c - 1)
+            quantise(1, CHUNKS - 1)
 
-        with tc.tile_pool(name="hidden", bufs=3) as hidden, tc.tile_pool(
+        with tc.tile_pool(name="hidden", bufs=4) as hidden, tc.tile_pool(
             name="outs", bufs=8
         ) as outs:
             h_tiles = {}
@@ -407,7 +466,6 @@ def tile_settransform_pa_t_kernel(
                     h_tiles[b] = hidden.tile([P, ROWS], F32, name="h")
                     stats1_tiles[b] = small.tile([P, CHUNKS, 6], F32, name="stats1")
                 h = h_tiles[b]
-                stats1 = stats1_tiles[b]
                 for c in range(half * RUN, (half + 1) * RUN):
                     cols = slice(c * CHUNK, (c + 1) * CHUNK)
                     acc = bank(BANKS + c % BANKS, [P, CHUNK], F32)
@@ -424,7 +482,7 @@ def tile_settransform_pa_t_kernel(
                     nc.scalar.activation(
                         out=h[:, cols], in_=acc[:], func=ACT.Relu, bias=params[:, b : b + 1]
                     )
-                    nc.vector.bn_stats(out=stats1[:, c, :], in_=h[:, cols])
+                    nc.vector.bn_stats(out=stats1_tiles[b][:, c, :], in_=h[:, cols])
 
             def normalise(b):
                 h = h_tiles[b]
@@ -433,15 +491,13 @@ def tile_settransform_pa_t_kernel(
                     out=moments1[:],
                     in_=stats1_tiles[b][:].rearrange("p c (s v) -> p (c s) v", v=3),
                 )
+                rstd = inverse_root(small, nc.gpsimd, moments1[:, 1:2])
                 scale1 = small.tile([P, 1], F32)
                 bias1 = small.tile([P, 1], F32)
-                norm_coefficients(
-                    nc,
+                scale_and_bias(
                     nc.gpsimd,
-                    small,
-                    neg_half,
                     moments1[:, 0:1],
-                    moments1[:, 1:2],
+                    rstd,
                     params[:, BLOCKS + b : BLOCKS + b + 1],
                     params[:, 2 * BLOCKS + b : 2 * BLOCKS + b + 1],
                     scale1[:],
@@ -457,26 +513,31 @@ def tile_settransform_pa_t_kernel(
                         op1=ALU.add,
                     )
 
-            def store_half(b, half):
+            def store_half(b, half, first_bank):
                 h = h_tiles[b]
                 for c in range(half * RUN, (half + 1) * RUN):
-                    o_ps = bank(c % BANKS, [P, ROW_TILES, P], F32)
+                    o_ps = bank(first_bank + c % BANKS, [P, ROW_TILES, P], F32)
                     for j in range(ROW_TILES):
                         lo = c * CHUNK + j * P
                         nc.tensor.transpose(
                             out=o_ps[:, j, :], in_=h[:, lo : lo + P], identity=ident_f32[:]
                         )
                     o_sb = outs.tile([P, ROW_TILES, P], F32)
-                    if c % 2 == 0:
+                    if c in V_COPIES:
                         nc.vector.tensor_copy(out=o_sb[:], in_=o_ps[:])
                     else:
                         nc.scalar.copy(out=o_sb[:], in_=o_ps[:])
                     nc.sync.dma_start(out=out_view[c][:, :, b * P : (b + 1) * P], in_=o_sb[:])
 
-            for k in range(2 * BLOCKS + LAG):
-                if k < 2 * BLOCKS:
-                    linear_half(k // 2, k % 2)
-                    if k % 2 == 1:
-                        normalise(k // 2)
-                if k >= LAG:
-                    store_half((k - LAG) // 2, (k - LAG) % 2)
+            runs = [(b, half) for b in range(BLOCKS) for half in range(2)]
+            made = 0
+            for k, (b, half) in enumerate(runs):
+                linear_half(b, half)
+                if half == 1:
+                    normalise(b)
+                wanted = max(0, k - LAG + 1) * (len(runs) - TAIL) // (len(runs) - LAG)
+                for b_out, half_out in runs[made:wanted]:
+                    store_half(b_out, half_out, 0)
+                made = max(made, wanted)
+            for b_out, half_out in runs[made:]:
+                store_half(b_out, half_out, half_out * BANKS)

@@ -103,6 +103,7 @@ def tile_settransform_pa_t_kernel(
             engine.tensor_mul(out=rstd[:], in0=mean, in1=scale_out)
             engine.tensor_sub(out=bias_out, in0=shift, in1=rstd[:])
 
+        h_tiles = {0: keep.tile([P, ROWS], F32, name="h_first")}
         with tc.tile_pool(name="early", bufs=1) as early, tc.tile_pool(
             name="xin", bufs=X_TILES
         ) as xin, tc.tile_pool(name="stage", bufs=11) as stage, tc.tile_pool(
@@ -454,16 +455,16 @@ def tile_settransform_pa_t_kernel(
                 quantise(1, c - 1)
             quantise(1, CHUNKS - 1)
 
-        with tc.tile_pool(name="hidden", bufs=4) as hidden, tc.tile_pool(
-            name="outs", bufs=8
+        with tc.tile_pool(name="hidden", bufs=3) as hidden, tc.tile_pool(
+            name="outs", bufs=16
         ) as outs:
-            h_tiles = {}
             stats1_tiles = {}
 
             def linear_half(b, half):
                 feats = slice(b * P, (b + 1) * P)
                 if half == 0:
-                    h_tiles[b] = hidden.tile([P, ROWS], F32, name="h")
+                    if b > 0:
+                        h_tiles[b] = hidden.tile([P, ROWS], F32, name="h")
                     stats1_tiles[b] = small.tile([P, CHUNKS, 6], F32, name="stats1")
                 h = h_tiles[b]
                 for c in range(half * RUN, (half + 1) * RUN):
@@ -493,24 +494,26 @@ def tile_settransform_pa_t_kernel(
                 )
                 rstd = inverse_root(small, nc.gpsimd, moments1[:, 1:2])
                 scale1 = small.tile([P, 1], F32)
-                bias1 = small.tile([P, 1], F32)
-                scale_and_bias(
-                    nc.gpsimd,
-                    moments1[:, 0:1],
-                    rstd,
-                    params[:, BLOCKS + b : BLOCKS + b + 1],
-                    params[:, 2 * BLOCKS + b : 2 * BLOCKS + b + 1],
-                    scale1[:],
-                    bias1[:],
+                drop1 = small.tile([P, 1], F32)
+                nc.gpsimd.tensor_mul(
+                    out=scale1[:], in0=params[:, BLOCKS + b : BLOCKS + b + 1], in1=rstd[:]
+                )
+                nc.gpsimd.tensor_scalar(
+                    out=drop1[:],
+                    in0=moments1[:, 0:1],
+                    scalar1=scale1[:, 0:1],
+                    scalar2=params[:, 2 * BLOCKS + b : 2 * BLOCKS + b + 1],
+                    op0=ALU.mult,
+                    op1=ALU.subtract,
                 )
                 for lo in range(0, ROWS, NORM_COLS):
                     nc.gpsimd.tensor_scalar(
                         out=h[:, lo : lo + NORM_COLS],
                         in0=h[:, lo : lo + NORM_COLS],
                         scalar1=scale1[:, 0:1],
-                        scalar2=bias1[:, 0:1],
+                        scalar2=drop1[:, 0:1],
                         op0=ALU.mult,
-                        op1=ALU.add,
+                        op1=ALU.subtract,
                     )
 
             def store_half(b, half, first_bank):

@@ -33,11 +33,11 @@ SCALAR_GROUPS = (1, 4, 5)
 WORD_BANKS = 3
 SUM_BANK = 3
 BANKS = 4
-NORM_COLS = 1024
+NORM_COLS = 2048
 RUN = 4
 LAG = 3
 TAIL = 4
-V_COPIES = (0, 2, 4, 6)
+V_COPIES = (0, 2, 5)
 EPS = 1e-5
 
 FLOPS = 2 * ROWS * D_IN * D_OUT
@@ -87,6 +87,7 @@ def tile_settransform_pa_t_kernel(
         x_codes = keep.tile([P, PASSES, ROWS], U32, align_bytes=64)
         x_scales = keep.tile([P, PASSES, ROWS], U8, align_bytes=64)
         params = keep.tile([P, 3 * BLOCKS], F32)
+        gains1 = keep.tile([P, BLOCKS, 2], F32)
 
         def inverse_root(pool, engine, var):
             rstd = pool.tile([P, var.shape[1]], F32, name="rstd")
@@ -446,6 +447,15 @@ def tile_settransform_pa_t_kernel(
             params_ps = bank(SUM_BANK, [P, 2 * CHUNK], BF16)
             nc.tensor.transpose(out=params_ps[:, 0:P], in_=param_rows[:], identity=ident_bf16[:])
             nc.vector.tensor_copy(out=params[:], in_=params_ps[:, 0 : 3 * BLOCKS])
+            for sign in range(2):
+                nc.gpsimd.tensor_scalar(
+                    out=gains1[:, :, sign],
+                    in0=params[:, BLOCKS : 2 * BLOCKS],
+                    scalar1=1.0 - 2.0 * sign,
+                    scalar2=0.0,
+                    op0=ALU.mult,
+                    op1=ALU.add,
+                )
 
             for c in range(1, CHUNKS):
                 for u in range(HALVES):
@@ -493,27 +503,27 @@ def tile_settransform_pa_t_kernel(
                     in_=stats1_tiles[b][:].rearrange("p c (s v) -> p (c s) v", v=3),
                 )
                 rstd = inverse_root(small, nc.gpsimd, moments1[:, 1:2])
-                scale1 = small.tile([P, 1], F32)
-                drop1 = small.tile([P, 1], F32)
+                scale1 = small.tile([P, 2], F32)
+                bias1 = small.tile([P, 1], F32)
                 nc.gpsimd.tensor_mul(
-                    out=scale1[:], in0=params[:, BLOCKS + b : BLOCKS + b + 1], in1=rstd[:]
+                    out=scale1[:], in0=gains1[:, b, :], in1=rstd[:].to_broadcast([P, 2])
                 )
                 nc.gpsimd.tensor_scalar(
-                    out=drop1[:],
+                    out=bias1[:],
                     in0=moments1[:, 0:1],
-                    scalar1=scale1[:, 0:1],
+                    scalar1=scale1[:, 1:2],
                     scalar2=params[:, 2 * BLOCKS + b : 2 * BLOCKS + b + 1],
                     op0=ALU.mult,
-                    op1=ALU.subtract,
+                    op1=ALU.add,
                 )
                 for lo in range(0, ROWS, NORM_COLS):
                     nc.gpsimd.tensor_scalar(
                         out=h[:, lo : lo + NORM_COLS],
                         in0=h[:, lo : lo + NORM_COLS],
                         scalar1=scale1[:, 0:1],
-                        scalar2=drop1[:, 0:1],
+                        scalar2=bias1[:, 0:1],
                         op0=ALU.mult,
-                        op1=ALU.subtract,
+                        op1=ALU.add,
                     )
 
             def store_half(b, half, first_bank):

@@ -113,8 +113,7 @@ def tile_settransform_pa_t_kernel(
             stats0 = early.tile([P, PASSES, PACK, len(BN_CHUNKS[0]), 6], F32)
             moments0 = early.tile([P, PASSES, PACK, 2], F32)
             natural = early.tile([P, PASSES, K_BLOCKS, 2], F32)
-            spread = early.tile([P, PASSES, K_BLOCKS * 2, PACK], F32)
-            part0 = early.tile([P, PASSES, 2, PACK], F32)
+            spread = early.tile([P, PASSES, (K_BLOCKS + 1) * 2, PACK], F32)
             total0 = early.tile([P, PASSES, 2, PACK], F32)
             square0 = early.tile([P, PASSES, PACK], F32)
             scale0 = early.tile([P, PASSES, PACK], F32)
@@ -195,8 +194,10 @@ def tile_settransform_pa_t_kernel(
                 return word_tiles[(g, c, u)][:].bitcast(BF16)[:, e : 2 * CHUNK : 2]
 
             def raw_planes(g, c, u):
-                for t in (2 * u, 2 * u + 1):
-                    nc.scalar.copy(out=planes_of(g, c)[:, t, :], in_=feature(g, c, t))
+                nc.scalar.copy(
+                    out=planes_of(g, c)[:, 2 * u : 2 * u + 2, :],
+                    in_=word_tiles[(g, c, u)][:].bitcast(BF16).rearrange("p (r e) -> p e r", e=2),
+                )
 
             def plane_statistics(g, c, t):
                 nc.vector.bn_stats(
@@ -212,10 +213,10 @@ def tile_settransform_pa_t_kernel(
                     )
                 share = count / CHUNKS
                 mean, var = moments0[:, g, :, 0], moments0[:, g, :, 1]
-                square = part0[:, g, 0, :]
+                square = spread[:, g, 2 * K_BLOCKS, :]
                 nc.gpsimd.tensor_mul(out=square, in0=mean, in1=mean)
                 nc.gpsimd.tensor_add(out=square, in0=square, in1=var)
-                for value, out_part in ((square, square), (mean, part0[:, g, 1, :])):
+                for value, out_part in ((square, square), (mean, spread[:, g, 2 * K_BLOCKS + 1, :])):
                     nc.gpsimd.tensor_scalar(
                         out=out_part, in0=value, scalar1=share, scalar2=0.0, op0=ALU.mult, op1=ALU.add
                     )
@@ -266,7 +267,7 @@ def tile_settransform_pa_t_kernel(
                     op=ALU.add,
                 )
                 nc.vector.tensor_mul(
-                    out=spread[:, g, :, :],
+                    out=spread[:, g, 0 : 2 * K_BLOCKS, :],
                     in0=natural[:, g, :, :]
                     .rearrange("p b v -> p (b v)")
                     .unsqueeze(2)
@@ -281,14 +282,14 @@ def tile_settransform_pa_t_kernel(
                 nc.tensor.matmul(
                     out=packed[:, 0 : K_BLOCKS * 2 * PACK],
                     lhsT=home[:].rearrange("p b i -> p (b i)"),
-                    rhs=spread[:, g, :, :].rearrange("p m t -> p (m t)"),
+                    rhs=spread[:, g, 0 : 2 * K_BLOCKS, :].rearrange("p m t -> p (m t)"),
                     start=True,
                     stop=True,
                 )
 
             def root_of(g):
                 nc.vector.tensor_mul(
-                    out=spread[:, g, :, :].rearrange("p (b v) t -> p b (v t)", v=2),
+                    out=spread[:, g, 0 : 2 * K_BLOCKS, :].rearrange("p (b v) t -> p b (v t)", v=2),
                     in0=word_tiles[(g, "packed")][:, 0 : K_BLOCKS * 2 * PACK].rearrange(
                         "p (b m) -> p b m", b=K_BLOCKS
                     ),
@@ -299,9 +300,6 @@ def tile_settransform_pa_t_kernel(
                     in_=spread[:, g, :, :].rearrange("p (b v) t -> p (v t) b", v=2),
                     axis=AXIS.X,
                     op=ALU.add,
-                )
-                nc.vector.tensor_add(
-                    out=total0[:, g, :, :], in0=total0[:, g, :, :], in1=part0[:, g, :, :]
                 )
                 mean, var = total0[:, g, 1, :], total0[:, g, 0, :]
                 nc.vector.tensor_mul(out=square0[:, g, :], in0=mean, in1=mean)
@@ -353,7 +351,8 @@ def tile_settransform_pa_t_kernel(
                 if on_scalar:
                     grouped = scalar_words.tile([P, CHUNK, PACK], BF16, align_bytes=64)
                     nc.scalar.copy(
-                        out=grouped[:], in_=planes_of(g, c)[:].rearrange("p t c -> p c t")
+                        out=grouped[:].rearrange("p (c i) t -> p c t i", i=4),
+                        in_=planes_of(g, c)[:].rearrange("p t (c i) -> p c t i", i=4),
                     )
                 else:
                     grouped = words.tile([P, CHUNK, PACK], BF16, align_bytes=64)

@@ -68,7 +68,7 @@ def tile_settransform_pa_t_kernel(
         neg_half = keep.tile([P, PACK], F32)
         nc.gpsimd.memset(neg_half[:], -0.5)
 
-        w_scales = keep.tile([P, PASSES, D_OUT], U8, align_bytes=64)
+        w_scales = keep.tile([P, PASSES, D_OUT], U8, align_bytes=256)
         nc.vector.memset(w_scales[:].rearrange("p g n -> p (g n)").bitcast(I32), 0)
         param_rows = keep.tile([P, P], BF16)
         nc.vector.memset(param_rows[:], 0.0)
@@ -83,9 +83,9 @@ def tile_settransform_pa_t_kernel(
                 in_=vec.rearrange("(b p) -> b p", p=P),
             )
 
-        w_codes = keep.tile([P, PASSES, D_OUT], U32, align_bytes=64)
-        x_codes = keep.tile([P, PASSES, ROWS], U32, align_bytes=64)
-        x_scales = keep.tile([P, PASSES, ROWS], U8, align_bytes=64)
+        w_codes = keep.tile([P, PASSES, D_OUT], U32, align_bytes=256)
+        x_codes = keep.tile([P, PASSES, ROWS], U32, align_bytes=256)
+        x_scales = keep.tile([P, PASSES, ROWS], U8, align_bytes=256)
         params = keep.tile([P, 3 * BLOCKS], F32)
         gains1 = keep.tile([P, BLOCKS, 2], F32)
 

from concourse import mybir
from concourse.masks import make_identity

F32 = mybir.dt.float32
BF16 = mybir.dt.bfloat16
I32 = mybir.dt.int32
U32 = mybir.dt.uint32
U8 = mybir.dt.uint8
FP8X4 = mybir.dt.float8_e4m3fn_x4
ACT = mybir.ActivationFunctionType
ALU = mybir.AluOpType
AXIS = mybir.AxisListType

P = 128
PACK = 4
K_PASS = P * PACK
ROWS = 4096
D_IN = 1024
D_OUT = 1024
PASSES = D_IN // K_PASS
CHUNK = 512
CHUNKS = ROWS // CHUNK
ROW_TILES = CHUNK // P
BLOCKS = D_OUT // P
K_BLOCKS = K_PASS // P
HALVES = 2
X_TILES = 13
BN_CHUNKS = ((0, 1, 2, 4), (0,))
SUM_CHUNKS = tuple(tuple(c for c in range(CHUNKS) if c not in bn) for bn in BN_CHUNKS)
RAW = (0, 1, 2, 4, 3, 5)
ORDER = RAW + (6, 7)
SCALAR_GROUPS = (1, 4, 5)
WORD_BANKS = 3
SUM_BANK = 3
BANKS = 4
NORM_COLS = 2048
RUN = 4
LAG = 3
TAIL = 4
V_COPIES = (0, 2, 5)
EPS = 1e-5

FLOPS = 2 * ROWS * D_IN * D_OUT


def tile_settransform_pa_t_kernel(
    tc, set_feats, g0, b0, W0_words, W0_scales, c0, g1, b1, out
):
    nc = tc.nc
    x_view = set_feats.flatten_outer_dims().rearrange(
        "(c p j) k -> c p j k", p=P, j=ROW_TILES
    )
    out_view = out.flatten_outer_dims().rearrange(
        "(c p j) n -> c p j n", p=P, j=ROW_TILES
    )

    with tc.tile_pool(name="keep", bufs=1) as keep, tc.tile_pool(
        name="small", bufs=4
    ) as small, tc.psum_pool(name="psum", bufs=1) as psum, tc.manual_schedule():

        def bank(i, shape, dtype):
            return psum.tile(shape, dtype, name="bank%d" % i)

        ident_f32 = keep.tile([P, P], F32)
        make_identity(nc, ident_f32[:])
        ident_bf16 = keep.tile([P, P], BF16)
        make_identity(nc, ident_bf16[:])
        neg_half = keep.tile([P, PACK], F32)
        nc.gpsimd.memset(neg_half[:], -0.5)

        w_scales = keep.tile([P, PASSES, D_OUT], U8, align_bytes=256)
        nc.vector.memset(w_scales[:].rearrange("p g n -> p (g n)").bitcast(I32), 0)
        param_rows = keep.tile([P, P], BF16)
        nc.vector.memset(param_rows[:], 0.0)

        gain0 = keep.tile([P, PASSES, PACK], BF16)
        shift0 = keep.tile([P, PASSES, PACK], BF16)
        nc.scalar.dma_start(out=gain0[:], in_=g0.rearrange("(g p t) -> p g t", g=PASSES, p=P))
        nc.scalar.dma_start(out=shift0[:], in_=b0.rearrange("(g p t) -> p g t", g=PASSES, p=P))
        for v, vec in enumerate((c0, g1, b1)):
            nc.scalar.dma_start(
                out=param_rows[v * BLOCKS : (v + 1) * BLOCKS, :],
                in_=vec.rearrange("(b p) -> b p", p=P),
            )

        w_codes = keep.tile([P, PASSES, D_OUT], U32, align_bytes=256)
        x_codes = keep.tile([P, PASSES, ROWS], U32, align_bytes=256)
        x_scales = keep.tile([P, PASSES, ROWS], U8, align_bytes=256)
        params = keep.tile([P, 3 * BLOCKS], F32)
        gains1 = keep.tile([P, BLOCKS, 2], F32)

        def inverse_root(pool, engine, var):
            rstd = pool.tile([P, var.shape[1]], F32, name="rstd")
            engine.tensor_scalar(
                out=rstd[:], in0=var, scalar1=0.0, scalar2=EPS, op0=ALU.max, op1=ALU.add
            )
            nc.gpsimd.tensor_tensor(
                out=rstd[:], in0=rstd[:], in1=neg_half[:, 0 : var.shape[1]], op=ALU.pow
            )
            return rstd

        def scale_and_bias(engine, mean, rstd, gain, shift, scale_out, bias_out):
            engine.tensor_mul(out=scale_out, in0=gain, in1=rstd[:])
            engine.tensor_mul(out=rstd[:], in0=mean, in1=scale_out)
            engine.tensor_sub(out=bias_out, in0=shift, in1=rstd[:])

        h_tiles = {0: keep.tile([P, ROWS], F32, name="h_first")}
        with tc.tile_pool(name="early", bufs=1) as early, tc.tile_pool(
            name="xin", bufs=X_TILES
        ) as xin, tc.tile_pool(name="stage", bufs=11) as stage, tc.tile_pool(
            name="words", bufs=3
        ) as words, tc.tile_pool(name="scalar_words", bufs=2) as scalar_words:
            stats0 = early.tile([P, PASSES, PACK, len(BN_CHUNKS[0]), 6], F32)
            moments0 = early.tile([P, PASSES, PACK, 2], F32)
            natural = early.tile([P, PASSES, K_BLOCKS, 2], F32)
            spread = early.tile([P, PASSES, (K_BLOCKS + 1) * 2, PACK], F32)
            total0 = early.tile([P, PASSES, 2, PACK], F32)
            square0 = early.tile([P, PASSES, PACK], F32)
            scale0 = early.tile([P, PASSES, PACK], F32)
            bias0 = early.tile([P, PASSES, PACK], F32)
            product = early.tile([P, P], F32)

            x_tiles = {}
            for g in range(PASSES):
                for c in range(CHUNKS):
                    x_sb = xin.tile([P, ROW_TILES, K_PASS], BF16, name="x_sb")
                    x_tiles[(g, c)] = x_sb
                    nc.sync.dma_start(
                        out=x_sb[:], in_=x_view[c][:, :, g * K_PASS : (g + 1) * K_PASS]
                    )
            for g in range(PASSES):
                nc.sync.dma_start(
                    out=w_codes[:, g, :].bitcast(I32),
                    in_=W0_words[g].rearrange("p n t -> p (n t)").bitcast(I32),
                )
            for g in range(PASSES):
                for q in range(4):
                    nc.sync.dma_start(
                        out=w_scales[32 * q : 32 * q + 4, g, :].bitcast(I32),
                        in_=W0_scales[g, 4 * q : 4 * q + 4, :].bitcast(I32),
                    )

            ones = early.tile([P, 2], BF16)
            nc.vector.memset(ones[:], 1.0)
            slot = early.tile([P, PACK], F32)
            nc.vector.tensor_reduce(
                out=slot[:],
                in_=ident_f32[:].rearrange("p (i t) -> p t i", t=PACK),
                axis=AXIS.X,
                op=ALU.add,
            )
            nc.vector.tensor_scalar(
                out=slot[:], in0=slot[:], scalar1=1.0 / ROWS, scalar2=0.0, op0=ALU.mult, op1=ALU.add
            )
            home = early.tile([P, K_BLOCKS, P // K_BLOCKS], F32)
            for b in range(K_BLOCKS):
                nc.vector.tensor_reduce(
                    out=home[:, b, :],
                    in_=ident_f32[:].rearrange("p (i t) -> p i t", t=PACK),
                    axis=AXIS.X,
                    op=ALU.add,
                )
            here = early.tile([P, K_BLOCKS], F32)
            nc.vector.tensor_reduce(
                out=here[:],
                in_=ident_f32[:].rearrange("p (b i) -> p b i", b=K_BLOCKS),
                axis=AXIS.X,
                op=ALU.add,
            )

            turns = []
            planes_tiles = {}
            grouped_tiles = {}
            word_tiles = {}

            def turn(g, c, u):
                x_ps = bank(len(turns) % WORD_BANKS, [P, CHUNK], F32)
                turns.append((g, c, u))
                word_tiles[(g, c, u)] = x_ps
                for j in range(ROW_TILES):
                    nc.tensor.transpose(
                        out=x_ps[:, j * P : (j + 1) * P],
                        in_=x_tiles[(g, c)][:, j, :].bitcast(F32)[:, u : K_PASS // 2 : HALVES],
                        identity=ident_f32[:],
                    )

            def planes_of(g, c):
                if (g, c) not in planes_tiles:
                    planes_tiles[(g, c)] = stage.tile([P, PACK, CHUNK], BF16, name="planes")
                return planes_tiles[(g, c)]

            def feature(g, c, t):
                u, e = divmod(t, 2)
                return word_tiles[(g, c, u)][:].bitcast(BF16)[:, e : 2 * CHUNK : 2]

            def raw_planes(g, c, u):
                nc.scalar.copy(
                    out=planes_of(g, c)[:, 2 * u : 2 * u + 2, :],
                    in_=word_tiles[(g, c, u)][:].bitcast(BF16).rearrange("p (r e) -> p e r", e=2),
                )

            def plane_statistics(g, c, t):
                nc.vector.bn_stats(
                    out=stats0[:, g, t, BN_CHUNKS[g].index(c), :], in_=planes_of(g, c)[:, t, :]
                )

            def first_part(g):
                count = len(BN_CHUNKS[g])
                for t in range(PACK):
                    nc.vector.bn_aggr(
                        out=moments0[:, g, t, :],
                        in_=stats0[:, g, t, 0:count, :].rearrange("p c (s v) -> p (c s) v", v=3),
                    )
                share = count / CHUNKS
                mean, var = moments0[:, g, :, 0], moments0[:, g, :, 1]
                square = spread[:, g, 2 * K_BLOCKS, :]
                nc.gpsimd.tensor_mul(out=square, in0=mean, in1=mean)
                nc.gpsimd.tensor_add(out=square, in0=square, in1=var)
                for value, out_part in ((square, square), (mean, spread[:, g, 2 * K_BLOCKS + 1, :])):
                    nc.gpsimd.tensor_scalar(
                        out=out_part, in0=value, scalar1=share, scalar2=0.0, op0=ALU.mult, op1=ALU.add
                    )

            def open_sums():
                squares = [bank(BANKS + b, [P, CHUNK], F32) for b in range(K_BLOCKS)]
                return squares, bank(SUM_BANK, [P, CHUNK], F32)

            def add_sums(g, c, b, banks):
                squares, sums = banks
                chunks = SUM_CHUNKS[g]
                column = b * CHUNKS + chunks.index(c)
                for j in range(ROW_TILES):
                    rows = x_tiles[(g, c)][:, j, b * P : (b + 1) * P]
                    nc.tensor.matmul(
                        out=squares[b][:, 0:P],
                        lhsT=rows,
                        rhs=rows,
                        start=(c == chunks[0] and j == 0),
                        stop=(c == chunks[-1] and j == ROW_TILES - 1),
                    )
                    nc.tensor.matmul(
                        out=sums[:, column : column + 1],
                        lhsT=rows,
                        rhs=ones[:, 0:1],
                        start=(j == 0),
                        stop=(j == ROW_TILES - 1),
                    )

            def read_sums(g, banks):
                squares, sums = banks
                for b in range(K_BLOCKS):
                    nc.vector.scalar_tensor_tensor(
                        out=product[:],
                        in0=squares[b][:, 0:P],
                        scalar=1.0,
                        in1=ident_f32[:],
                        op0=ALU.mult,
                        op1=ALU.mult,
                        accum_out=natural[:, g, b, 0:1],
                    )
                nc.vector.tensor_reduce(
                    out=natural[:, g, :, 1],
                    in_=sums[:, 0 : K_BLOCKS * CHUNKS].rearrange("p (b c) -> p b c", c=CHUNKS)[
                        :, :, 0 : len(SUM_CHUNKS[g])
                    ],
                    axis=AXIS.X,
                    op=ALU.add,
                )
                nc.vector.tensor_mul(
                    out=spread[:, g, 0 : 2 * K_BLOCKS, :],
                    in0=natural[:, g, :, :]
                    .rearrange("p b v -> p (b v)")
                    .unsqueeze(2)
                    .to_broadcast([P, K_BLOCKS * 2, PACK]),
                    in1=slot[:].unsqueeze(1).to_broadcast([P, K_BLOCKS * 2, PACK]),
                )

            def pack_sums(g):
                packed = bank(len(turns) % WORD_BANKS, [P, CHUNK], F32)
                turns.append("packed")
                word_tiles[(g, "packed")] = packed
                nc.tensor.matmul(
                    out=packed[:, 0 : K_BLOCKS * 2 * PACK],
                    lhsT=home[:].rearrange("p b i -> p (b i)"),
                    rhs=spread[:, g, 0 : 2 * K_BLOCKS, :].rearrange("p m t -> p (m t)"),
                    start=True,
                    stop=True,
                )

            def root_of(g):
                nc.vector.tensor_mul(
                    out=spread[:, g, 0 : 2 * K_BLOCKS, :].rearrange("p (b v) t -> p b (v t)", v=2),
                    in0=word_tiles[(g, "packed")][:, 0 : K_BLOCKS * 2 * PACK].rearrange(
                        "p (b m) -> p b m", b=K_BLOCKS
                    ),
                    in1=here[:].unsqueeze(2).to_broadcast([P, K_BLOCKS, 2 * PACK]),
                )
                nc.vector.tensor_reduce(
                    out=total0[:, g, :, :].rearrange("p v t -> p (v t)"),
                    in_=spread[:, g, :, :].rearrange("p (b v) t -> p (v t) b", v=2),
                    axis=AXIS.X,
                    op=ALU.add,
                )
                mean, var = total0[:, g, 1, :], total0[:, g, 0, :]
                nc.vector.tensor_mul(out=square0[:, g, :], in0=mean, in1=mean)
                nc.vector.tensor_sub(out=var, in0=var, in1=square0[:, g, :])
                return inverse_root(early, nc.vector, var)

            def coefficients(g, rstd):
                scale_and_bias(
                    nc.vector,
                    total0[:, g, 1, :],
                    rstd,
                    gain0[:, g, :],
                    shift0[:, g, :],
                    scale0[:, g, :],
                    bias0[:, g, :],
                )

            def affine_planes(g, c):
                for t in range(PACK):
                    plane = planes_of(g, c)[:, t, :]
                    nc.vector.tensor_scalar(
                        out=plane,
                        in0=plane,
                        scalar1=scale0[:, g, t : t + 1],
                        scalar2=bias0[:, g, t : t + 1],
                        op0=ALU.mult,
                        op1=ALU.add,
                    )

            def affine_bank(g, c, u):
                for t in (2 * u, 2 * u + 1):
                    nc.scalar.activation(
                        out=planes_of(g, c)[:, t, :],
                        in_=feature(g, c, t),
                        func=ACT.Identity,
                        scale=scale0[:, g, t : t + 1],
                        bias=bias0[:, g, t : t + 1],
                    )

            def quantise(g, c):
                cols = slice(c * CHUNK, (c + 1) * CHUNK)
                nc.vector.quantize_mx(
                    out=x_codes[:, g, cols].bitcast(FP8X4),
                    scales=x_scales[:, g, cols],
                    in_=grouped_tiles[(g, c)][:].rearrange("p c t -> p (c t)"),
                )

            def group(g, c, on_scalar):
                if on_scalar:
                    grouped = scalar_words.tile([P, CHUNK, PACK], BF16, align_bytes=64)
                    nc.scalar.copy(
                        out=grouped[:].rearrange("p (c i) t -> p c t i", i=4),
                        in_=planes_of(g, c)[:].rearrange("p t (c i) -> p c t i", i=4),
                    )
                else:
                    grouped = words.tile([P, CHUNK, PACK], BF16, align_bytes=64)
                    nc.vector.tensor_copy(
                        out=grouped[:].rearrange("p (c i) t -> p c t i", i=4),
                        in_=planes_of(g, c)[:].rearrange("p t (c i) -> p c t i", i=4),
                    )
                grouped_tiles[(g, c)] = grouped

            banks0 = open_sums()
            for c in range(CHUNKS):
                if c in BN_CHUNKS[0]:
                    for u in range(HALVES):
                        turn(0, c, u)
                        raw_planes(0, c, u)
                        for t in (2 * u, 2 * u + 1):
                            plane_statistics(0, c, t)
                else:
                    for b in range(K_BLOCKS):
                        add_sums(0, c, b, banks0)
            first_part(0)
            read_sums(0, banks0)
            banks1 = open_sums()
            left = [(c, b) for c in SUM_CHUNKS[1] for b in range(K_BLOCKS)]

            def sums1(lo, hi):
                for c, b in left[lo:hi]:
                    add_sums(1, c, b, banks1)

            turn(1, 0, 0)
            turn(1, 0, 1)
            sums1(0, 4)
            pack_sums(0)
            raw_planes(1, 0, 0)
            raw_planes(1, 0, 1)
            plane_statistics(1, 0, 0)
            rstd0 = root_of(0)
            turn(0, 3, 0)
            turn(0, 3, 1)
            raw_planes(0, 3, 0)
            raw_planes(0, 3, 1)
            plane_statistics(1, 0, 1)
            plane_statistics(1, 0, 2)
            coefficients(0, rstd0)
            sums1(4, 12)
            turn(0, 5, 0)
            turn(0, 5, 1)
            raw_planes(0, 5, 0)
            raw_planes(0, 5, 1)
            sums1(12, 16)
            sums1(16, len(left))
            turn(0, 6, 0)
            turn(0, 6, 1)
            affine_planes(0, 0)
            affine_planes(0, 1)
            group(0, 0, False)
            group(0, 1, True)
            affine_planes(0, 2)
            affine_planes(0, 4)
            group(0, 2, False)
            group(0, 4, True)
            quantise(0, 0)
            affine_planes(0, 3)
            affine_bank(0, 6, 0)
            affine_bank(0, 6, 1)
            quantise(0, 1)
            plane_statistics(1, 0, 3)
            first_part(1)
            read_sums(1, banks1)
            pack_sums(1)
            turn(0, 7, 0)
            turn(0, 7, 1)
            group(0, 3, False)
            rstd1 = root_of(1)
            affine_bank(0, 7, 0)
            affine_bank(0, 7, 1)
            affine_planes(0, 5)
            quantise(0, 2)
            quantise(0, 4)
            coefficients(1, rstd1)
            group(0, 5, True)
            affine_planes(1, 0)
            group(0, 6, False)
            quantise(0, 3)
            group(0, 7, False)
            quantise(0, 6)
            group(1, 0, False)
            quantise(0, 7)
            quantise(0, 5)

            params_ps = bank(SUM_BANK, [P, 2 * CHUNK], BF16)
            nc.tensor.transpose(out=params_ps[:, 0:P], in_=param_rows[:], identity=ident_bf16[:])
            nc.vector.tensor_copy(out=params[:], in_=params_ps[:, 0 : 3 * BLOCKS])
            for sign in range(2):
                nc.gpsimd.tensor_scalar(
                    out=gains1[:, :, sign],
                    in0=params[:, BLOCKS : 2 * BLOCKS],
                    scalar1=1.0 - 2.0 * sign,
                    scalar2=0.0,
                    op0=ALU.mult,
                    op1=ALU.add,
                )

            for c in range(1, CHUNKS):
                for u in range(HALVES):
                    turn(1, c, u)
                    affine_bank(1, c, u)
                group(1, c, False)
                quantise(1, c - 1)
            quantise(1, CHUNKS - 1)

        with tc.tile_pool(name="hidden", bufs=3) as hidden, tc.tile_pool(
            name="outs", bufs=16
        ) as outs:
            stats1_tiles = {}

            def linear_half(b, half):
                feats = slice(b * P, (b + 1) * P)
                if half == 0:
                    if b > 0:
                        h_tiles[b] = hidden.tile([P, ROWS], F32, name="h")
                    stats1_tiles[b] = small.tile([P, CHUNKS, 6], F32, name="stats1")
                h = h_tiles[b]
                for c in range(half * RUN, (half + 1) * RUN):
                    cols = slice(c * CHUNK, (c + 1) * CHUNK)
                    acc = bank(BANKS + c % BANKS, [P, CHUNK], F32)
                    for g in range(PASSES):
                        nc.tensor.matmul_mx(
                            out=acc[:],
                            lhsT=w_codes[:, g, feats].bitcast(FP8X4),
                            lhsT_scale=w_scales[:, g, feats],
                            rhs=x_codes[:, g, cols].bitcast(FP8X4),
                            rhs_scale=x_scales[:, g, cols],
                            start=(g == 0),
                            stop=(g == PASSES - 1),
                        )
                    nc.scalar.activation(
                        out=h[:, cols], in_=acc[:], func=ACT.Relu, bias=params[:, b : b + 1]
                    )
                    nc.vector.bn_stats(out=stats1_tiles[b][:, c, :], in_=h[:, cols])

            def normalise(b):
                h = h_tiles[b]
                moments1 = small.tile([P, 2], F32)
                nc.vector.bn_aggr(
                    out=moments1[:],
                    in_=stats1_tiles[b][:].rearrange("p c (s v) -> p (c s) v", v=3),
                )
                rstd = inverse_root(small, nc.gpsimd, moments1[:, 1:2])
                scale1 = small.tile([P, 2], F32)
                bias1 = small.tile([P, 1], F32)
                nc.gpsimd.tensor_mul(
                    out=scale1[:], in0=gains1[:, b, :], in1=rstd[:].to_broadcast([P, 2])
                )
                nc.gpsimd.tensor_scalar(
                    out=bias1[:],
                    in0=moments1[:, 0:1],
                    scalar1=scale1[:, 1:2],
                    scalar2=params[:, 2 * BLOCKS + b : 2 * BLOCKS + b + 1],
                    op0=ALU.mult,
                    op1=ALU.add,
                )
                for lo in range(0, ROWS, NORM_COLS):
                    nc.gpsimd.tensor_scalar(
                        out=h[:, lo : lo + NORM_COLS],
                        in0=h[:, lo : lo + NORM_COLS],
                        scalar1=scale1[:, 0:1],
                        scalar2=bias1[:, 0:1],
                        op0=ALU.mult,
                        op1=ALU.add,
                    )

            def store_half(b, half, first_bank):
                h = h_tiles[b]
                for c in range(half * RUN, (half + 1) * RUN):
                    o_ps = bank(first_bank + c % BANKS, [P, ROW_TILES, P], F32)
                    for j in range(ROW_TILES):
                        lo = c * CHUNK + j * P
                        nc.tensor.transpose(
                            out=o_ps[:, j, :], in_=h[:, lo : lo + P], identity=ident_f32[:]
                        )
                    o_sb = outs.tile([P, ROW_TILES, P], F32)
                    if c in V_COPIES:
                        nc.vector.tensor_copy(out=o_sb[:], in_=o_ps[:])
                    else:
                        nc.scalar.copy(out=o_sb[:], in_=o_ps[:])
                    nc.sync.dma_start(out=out_view[c][:, :, b * P : (b + 1) * P], in_=o_sb[:])

            runs = [(b, half) for b in range(BLOCKS) for half in range(2)]
            made = 0
            for k, (b, half) in enumerate(runs):
                linear_half(b, half)
                if half == 1:
                    normalise(b)
                wanted = max(0, k - LAG + 1) * (len(runs) - TAIL) // (len(runs) - LAG)
                for b_out, half_out in runs[made:wanted]:
                    store_half(b_out, half_out, 0)
                made = max(made, wanted)
            for b_out, half_out in runs[made:]:
                store_half(b_out, half_out, half_out * BANKS)
